import numpy as np
import ml_dtypes


def mxq(x, axis, fmt="e4m3"):
    dtype, down = {"e4m3": (ml_dtypes.float8_e4m3fn, 7), "e5m2": (ml_dtypes.float8_e5m2, 14)}[fmt]
    v = np.moveaxis(np.asarray(x, np.float32).astype(ml_dtypes.bfloat16).astype(np.float64), axis, -1)
    blocks = v.reshape(v.shape[:-1] + (-1, 32))
    amax = np.abs(blocks).max(-1, keepdims=True)
    byte = np.maximum(np.where(amax > 0, np.frexp(amax)[1] - 1 + 127, 0) - down, 1)
    scale = np.exp2(byte - 127.0)
    codes = (blocks / scale).astype(np.float32).astype(dtype).astype(np.float64)
    return np.moveaxis((codes * scale).reshape(v.shape), -1, axis)


WIDE = False


def mx_kscale(k):
    if not WIDE:
        return np.ones(k)
    levels = np.array([10, -10, 5, -5, 0])
    a = np.random.permutation(np.resize(levels, k // 512 * 4)).reshape(k // 512, 4)
    idx = np.arange(k)
    return np.exp2(a[idx // 512, idx % 128 // 32])


BF16 = ml_dtypes.bfloat16


def bf(x):
    return np.asarray(x, np.float32).astype(BF16)


def f64(x):
    return np.asarray(x).astype(np.float64)


E2M1 = np.array([0.0, 0.5, 1.0, 1.5, 2.0, 3.0, 4.0, 6.0, -0.0, -0.5, -1.0, -1.5, -2.0, -3.0, -4.0, -6.0])


def pack_weight(w, fmt):
    k, n = w.shape
    w = f64(bf(w)).reshape(k // 32, 32, n)
    amax = np.abs(w).max(1)
    if fmt == "e4m3":
        byte = np.frexp(amax)[1] - 1 + 127 - 7
    else:
        mant, ex = np.frexp(amax / 6.0)
        byte = np.where(mant > 0.5, ex, ex - 1) + 127
    byte = np.clip(np.where(amax > 0, byte, 1), 1, 254)
    scaled = (w * np.exp2(127.0 - byte)[:, None, :]).reshape(k, n).astype(np.float32)
    by_word = np.ascontiguousarray(scaled.reshape(k // 512, 128, 4, n).transpose(0, 1, 3, 2))
    if fmt == "e4m3":
        words = by_word.astype(ml_dtypes.float8_e4m3fn).view(np.uint8)
    else:
        c = by_word.astype(ml_dtypes.float4_e2m1fn).view(np.uint8) & 0xF
        words = c[..., 0::2] | (c[..., 1::2] << 4)
    return np.ascontiguousarray(words), np.ascontiguousarray(byte.astype(np.uint8).reshape(k // 512, 16, n))


def unpack_weight(words, scales, fmt):
    g, p, n, _ = words.shape
    if fmt == "e4m3":
        vals = np.ascontiguousarray(words).view(ml_dtypes.float8_e4m3fn).astype(np.float64)
    else:
        nib = np.empty((g, p, n, 4), np.uint8)
        nib[..., 0::2] = words & 0xF
        nib[..., 1::2] = words >> 4
        vals = E2M1[nib]
    vals = vals * np.repeat(np.exp2(scales.astype(np.float64) - 127.0), 8, axis=1)[..., None]
    return vals.transpose(0, 1, 3, 2).reshape(g * 512, n)

def pack4(w):
    words, scales = pack_weight(w, "e2m1")
    return words.reshape(words.shape[0], 128, -1), scales


def unpack4(words, scales):
    return unpack_weight(words.reshape(words.shape[0], 128, -1, 2), scales, "e2m1")


B, S, HID, NH, NOPE, ROPE, VD, KV_RANK, SW, QB = 1, 2048, 1024, 8, 64, 128, 128, 512, 384, 128
QK = NOPE + ROPE


def rotate_half(x):
    h = x.shape[-1] // 2
    return np.concatenate([-x[..., h:], x[..., :h]], axis=-1)


def rope_tables():
    pos = np.arange(S, dtype=np.float64)
    inv = 1.0 / (10000.0 ** (np.arange(0, ROPE, 2, dtype=np.float64) / ROPE))
    ang = pos[:, None] * inv[None, :]
    ang = np.concatenate([ang, ang], axis=-1)
    return bf(np.broadcast_to(np.cos(ang)[None], (B, S, ROPE))), bf(np.broadcast_to(np.sin(ang)[None], (B, S, ROPE)))


def setup_inputs():
    s = mx_kscale(HID)
    cos, sin = rope_tables()
    hidden_states = bf(np.random.standard_normal((B, S, HID)) * s)
    Wq_words, Wq_scales = pack4(np.random.standard_normal((HID, NH * QK)) * 2.0 / np.sqrt(HID) / s[:, None])
    bq = bf(np.random.standard_normal(NH * QK) * 0.2)
    return {"hidden_states": hidden_states, "cos": cos, "sin": sin,
            "Wq_words": Wq_words, "Wq_scales": Wq_scales,
            "bq": bq}


def reference(hidden_states, cos, sin, Wq_words, Wq_scales, bq):
    q = ((mxq(f64(hidden_states), 2, "e4m3") @ unpack4(Wq_words, Wq_scales)) + f64(bq)).reshape(B, S, NH, QK).transpose(0, 2, 1, 3)
    q_nope, q_rope = q[..., :NOPE], q[..., NOPE:]
    c, si = f64(cos)[:, None], f64(sin)[:, None]
    q_rope = q_rope * c + rotate_half(q_rope) * si
    return np.concatenate([q_nope, q_rope], axis=-1)

@@ -1,0 +1,230 @@
+import concourse.mybir as mybir
+from concourse.masks import make_identity
+
+F32 = mybir.dt.float32
+BF16 = mybir.dt.bfloat16
+I32 = mybir.dt.int32
+U32 = mybir.dt.uint32
+U8 = mybir.dt.uint8
+FP8X4 = mybir.dt.float8_e4m3fn_x4
+FP4X4 = mybir.dt.float4_e2m1fn_x4
+ADD = mybir.AluOpType.add
+MULT = mybir.AluOpType.mult
+
+P = 128
+SEQ = 2048
+HID = 1024
+HEADS = 8
+NOPE = 64
+ROPE = 128
+HALF = ROPE // 2
+HEAD = NOPE + ROPE
+COLS = HEADS * HEAD
+K_PASS = 4 * P
+PASSES = HID // K_PASS
+BANK = 512
+BANKS = COLS // BANK
+HEADS_PER_BANK = BANK // ROPE
+ROPE_BANKS = HEADS // HEADS_PER_BANK
+TILES = SEQ // P
+TILES_PER_STORE = 2
+
+FLOPS = 2 * SEQ * HID * COLS
+
+
+def sort_columns(nc, sorted_bytes, raw_bytes, bytes_per_column):
+    nope_words = NOPE * bytes_per_column // 4
+    head_words = HEAD * bytes_per_column // 4
+    raw = raw_bytes.bitcast(I32).rearrange("p g (h c) -> p g h c", h=HEADS)
+    tidy = sorted_bytes.bitcast(I32)
+    split = HEADS * (head_words - nope_words)
+    nc.vector.tensor_copy(
+        out=tidy[:, :, 0:split].rearrange("p g (h c) -> p g h c", h=HEADS),
+        in_=raw[:, :, :, nope_words:head_words],
+    )
+    nc.vector.tensor_copy(
+        out=tidy[:, :, split:].rearrange("p g (h c) -> p g h c", h=HEADS),
+        in_=raw[:, :, :, 0:nope_words],
+    )
+
+
+def tile_gptossmlaattention_pb_kernel(tc, hidden_states, cos, sin, Wq_words, Wq_scales, bq, out):
+    nc = tc.nc
+    x_dram = hidden_states[0].rearrange("(p t) k -> p t k", t=TILES)
+    cos_dram = cos[0].rearrange("(p t) d -> p t d", t=TILES)
+    sin_dram = sin[0].rearrange("(p t) d -> p t d", t=TILES)
+    out_dram = out[0].rearrange("h (p t) d -> p h t d", t=TILES)
+
+    with tc.tile_pool(name="keep", bufs=1) as keep, tc.tile_pool(name="words", bufs=4) as words, tc.tile_pool(
+        name="scratch", bufs=3
+    ) as scratch, tc.tile_pool(name="results", bufs=4) as results, tc.psum_pool(
+        name="turned", bufs=1
+    ) as turned, tc.psum_pool(name="tables", bufs=1) as tables, tc.psum_pool(
+        name="sums", bufs=2
+    ) as sums, tc.manual_schedule():
+        x_sb = keep.tile([P, TILES, HID], BF16)
+        w_raw = keep.tile([P, PASSES, 2 * COLS], U8)
+        w_words = keep.tile([P, PASSES, 2 * COLS], U8, align_bytes=64)
+        scale_raw = keep.tile([P, PASSES, COLS], U8)
+        w_scales = keep.tile([P, PASSES, COLS], U8, align_bytes=64)
+        bias_row = keep.tile([P, COLS], BF16)
+        ones = keep.tile([P, P], BF16)
+        bias = keep.tile([P, COLS], F32)
+        angles = keep.tile([P, 2, TILES, ROPE], BF16)
+        identity = keep.tile([P, P], F32)
+        identity_bf = keep.tile([P, P], BF16)
+
+        nc.vector.memset(bias_row[:].bitcast(I32), 0)
+        nc.vector.memset(scale_raw[:].bitcast(I32), 0)
+        nc.vector.memset(ones[:], 1.0)
+        make_identity(nc, identity[:])
+        make_identity(nc, identity_bf[:])
+
+        def load_x(tiles):
+            nc.sync.dma_start(out=x_sb[:, tiles, :], in_=x_dram[:, tiles, :])
+
+        def load_angles(tiles):
+            nc.sync.dma_start(out=angles[:, 0, tiles, :], in_=cos_dram[:, tiles, :])
+            nc.sync.dma_start(out=angles[:, 1, tiles, :], in_=sin_dram[:, tiles, :])
+
+        early = slice(0, 4)
+        late = slice(4, TILES)
+        load_x(slice(0, 1))
+        nc.sync.dma_start(out=bias_row[0:1, :], in_=bq.unsqueeze(0))
+        for r in range(4):
+            nc.sync.dma_start(
+                out=scale_raw[r:P:32].bitcast(I32),
+                in_=Wq_scales[:, r:16:4, :].rearrange("g q n -> q g n").bitcast(I32),
+            )
+        nc.sync.dma_start(out=w_raw[:].bitcast(I32), in_=Wq_words.rearrange("g p n -> p g n").bitcast(I32))
+        load_x(slice(1, 2))
+        load_angles(early)
+        load_x(slice(2, 4))
+        load_angles(late)
+        for first in range(4, TILES, 2):
+            load_x(slice(first, first + 2))
+
+        bias_by_head = bias[:].rearrange("p (h d) -> p h d", h=HEADS)
+
+        def new_banks():
+            banks = []
+            for b in range(BANKS):
+                bank = sums.tile([P, BANK], F32, name="bank%d" % b)
+                banks.append(bank)
+            return banks
+
+        def spread_bias():
+            banks = new_banks()
+            for b in range(BANKS):
+                columns = slice(b * BANK, (b + 1) * BANK)
+                nc.tensor.matmul(out=banks[b][:], lhsT=ones[:], rhs=bias_row[:, columns], start=True, stop=True)
+                nc.scalar.copy(out=bias[:, columns], in_=banks[b][:])
+
+        def negate_first_half_of_sin(tiles):
+            nc.scalar.mul(out=angles[:, 1, tiles, 0:HALF], in_=angles[:, 1, tiles, 0:HALF], mul=-1.0)
+
+        def angles_to_psum(t):
+            table = tables.tile([P, 2, ROPE], F32)
+            nc.tensor.matmul(out=table[:], lhsT=identity_bf[:], rhs=angles[:, :, t, :], start=True, stop=True)
+            return table
+
+        def turn_tile(t):
+            x_words = x_sb[:, t, :].bitcast(F32)
+            flipped = turned.tile([P, 2 * PASSES, P], F32)
+            for g in range(PASSES):
+                for u in range(2):
+                    first = g * (K_PASS // 2) + u
+                    nc.tensor.transpose(flipped[:, 2 * g + u, :], x_words[:, first : (g + 1) * (K_PASS // 2) : 2], identity[:])
+            grouped = words.tile([P, PASSES * P * 4], BF16, align_bytes=64)
+            nc.scalar.copy(
+                out=grouped[:].bitcast(F32).rearrange("p (g r u) -> p g r u", g=PASSES, u=2),
+                in_=flipped[:].rearrange("p (g u) r -> p g r u", u=2),
+            )
+            return grouped
+
+        def quantise_tile(grouped):
+            codes = words.tile([P, PASSES * P], U32, align_bytes=64)
+            code_scales = words.tile([P, PASSES * P], U8, align_bytes=64)
+            nc.vector.quantize_mx(out=codes[:].bitcast(FP8X4), scales=code_scales[:], in_=grouped[:])
+            return codes, code_scales
+
+        def multiply_tile(codes, code_scales):
+            banks = new_banks()
+            for b in range(BANKS):
+                for g in range(PASSES):
+                    nc.tensor.matmul_mx(
+                        out=banks[b][:],
+                        lhsT=codes[:, g * P : (g + 1) * P].bitcast(FP8X4),
+                        lhsT_scale=code_scales[:, g * P : (g + 1) * P],
+                        rhs=w_words[:, g, 2 * b * BANK : 2 * (b + 1) * BANK].bitcast(FP4X4),
+                        rhs_scale=w_scales[:, g, b * BANK : (b + 1) * BANK],
+                        start=(g == 0),
+                        stop=(g == PASSES - 1),
+                    )
+            return banks
+
+        def finish_tile(banks, table, result):
+            nc.scalar.copy(out=result[:, :, 0:NOPE], in_=banks[ROPE_BANKS][:].rearrange("p (h d) -> p h d", h=HEADS))
+            nc.gpsimd.tensor_tensor(
+                out=result[:, :, 0:NOPE], in0=result[:, :, 0:NOPE], in1=bias_by_head[:, :, 0:NOPE], op=ADD
+            )
+            x = scratch.tile([P, HEADS, ROPE], F32)
+            for b in range(ROPE_BANKS):
+                heads = slice(b * HEADS_PER_BANK, (b + 1) * HEADS_PER_BANK)
+                nc.vector.tensor_tensor(
+                    out=x[:, heads, :],
+                    in0=banks[b][:].rearrange("p (h d) -> p h d", h=HEADS_PER_BANK),
+                    in1=bias_by_head[:, heads, NOPE:HEAD],
+                    op=ADD,
+                )
+            nc.vector.tensor_tensor(
+                out=result[:, :, NOPE:HEAD],
+                in0=x[:],
+                in1=table[:, 0, :].unsqueeze(1).to_broadcast([P, HEADS, ROPE]),
+                op=MULT,
+            )
+            crossed = scratch.tile([P, HEADS, ROPE], F32)
+            for f in range(2):
+                here = slice(f * HALF, (f + 1) * HALF)
+                there = slice((1 - f) * HALF, (2 - f) * HALF)
+                nc.vector.tensor_tensor(
+                    out=crossed[:, :, here],
+                    in0=x[:, :, there],
+                    in1=table[:, 1, here].unsqueeze(1).to_broadcast([P, HEADS, HALF]),
+                    op=MULT,
+                )
+            nc.gpsimd.tensor_tensor(out=result[:, :, NOPE:HEAD], in0=result[:, :, NOPE:HEAD], in1=crossed[:], op=ADD)
+
+        def store_tile(t, result):
+            place = t % TILES_PER_STORE
+            if t >= TILES - TILES_PER_STORE:
+                nc.sync.dma_start(out=out_dram[:, :, t, :], in_=result[:, :, place, :])
+            elif place == TILES_PER_STORE - 1:
+                nc.sync.dma_start(out=out_dram[:, :, t + 1 - TILES_PER_STORE : t + 1, :], in_=result[:])
+
+        quantised = {}
+        banks = {}
+        quantised[0] = quantise_tile(turn_tile(0))
+        spread_bias()
+        sort_columns(nc, w_scales[:], scale_raw[:], 1)
+        sort_columns(nc, w_words[:], w_raw[:], 2)
+        quantised[1] = quantise_tile(turn_tile(1))
+        negate_first_half_of_sin(early)
+        banks[0] = multiply_tile(*quantised[0])
+
+        result = None
+        for t in range(TILES):
+            table = angles_to_psum(t)
+            grouped = None
+            if t + 2 < TILES:
+                grouped = turn_tile(t + 2)
+            if t + 1 < TILES:
+                banks[t + 1] = multiply_tile(*quantised[t + 1])
+            if t % TILES_PER_STORE == 0:
+                result = results.tile([P, HEADS, TILES_PER_STORE, HEAD], F32)
+            finish_tile(banks[t], table, result[:, :, t % TILES_PER_STORE, :])
+            store_tile(t, result)
+            if t + 2 < TILES:
+                quantised[t + 2] = quantise_tile(grouped)
+            if t == 0:
+                negate_first_half_of_sin(late)

@@ -1,3 +1,5 @@
+from contextlib import ExitStack
+
 import concourse.mybir as mybir
 from concourse.masks import make_identity
 
@@ -10,6 +12,7 @@ FP8X4 = mybir.dt.float8_e4m3fn_x4
 FP4X4 = mybir.dt.float4_e2m1fn_x4
 ADD = mybir.AluOpType.add
 MULT = mybir.AluOpType.mult
+IDENTITY = mybir.ActivationFunctionType.Identity
 
 P = 128
 SEQ = 2048
@@ -22,30 +25,14 @@ HEAD = NOPE + ROPE
 COLS = HEADS * HEAD
 K_PASS = 4 * P
 PASSES = HID // K_PASS
-BANK = 512
-BANKS = COLS // BANK
-HEADS_PER_BANK = BANK // ROPE
-ROPE_BANKS = HEADS // HEADS_PER_BANK
 TILES = SEQ // P
-TILES_PER_STORE = 2
+BLOCK = 4
+BLOCKS = TILES // BLOCK
+SLOTS_PER_BLOCK = HEADS // 2
+SLOTS = BLOCKS * SLOTS_PER_BLOCK
+NOPE_LEAD = 2
 
 FLOPS = 2 * SEQ * HID * COLS
-
-
-def sort_columns(nc, sorted_bytes, raw_bytes, bytes_per_column):
-    nope_words = NOPE * bytes_per_column // 4
-    head_words = HEAD * bytes_per_column // 4
-    raw = raw_bytes.bitcast(I32).rearrange("p g (h c) -> p g h c", h=HEADS)
-    tidy = sorted_bytes.bitcast(I32)
-    split = HEADS * (head_words - nope_words)
-    nc.vector.tensor_copy(
-        out=tidy[:, :, 0:split].rearrange("p g (h c) -> p g h c", h=HEADS),
-        in_=raw[:, :, :, nope_words:head_words],
-    )
-    nc.vector.tensor_copy(
-        out=tidy[:, :, split:].rearrange("p g (h c) -> p g h c", h=HEADS),
-        in_=raw[:, :, :, 0:nope_words],
-    )
 
 
 def tile_gptossmlaattention_pb_kernel(tc, hidden_states, cos, sin, Wq_words, Wq_scales, bq, out):
@@ -55,30 +42,41 @@ def tile_gptossmlaattention_pb_kernel(tc, hidden_states, cos, sin, Wq_words, Wq_
     sin_dram = sin[0].rearrange("(p t) d -> p t d", t=TILES)
     out_dram = out[0].rearrange("h (p t) d -> p h t d", t=TILES)
 
-    with tc.tile_pool(name="keep", bufs=1) as keep, tc.tile_pool(name="words", bufs=4) as words, tc.tile_pool(
-        name="scratch", bufs=3
-    ) as scratch, tc.tile_pool(name="results", bufs=4) as results, tc.psum_pool(
-        name="turned", bufs=1
-    ) as turned, tc.psum_pool(name="tables", bufs=1) as tables, tc.psum_pool(
-        name="sums", bufs=2
-    ) as sums, tc.manual_schedule():
+    with ExitStack() as ctx:
+        keep = ctx.enter_context(tc.tile_pool(name="keep", bufs=1))
+        staging = ctx.enter_context(tc.tile_pool(name="staging", bufs=3))
+        channels = ctx.enter_context(tc.tile_pool(name="channels", bufs=4))
+        scratch = ctx.enter_context(tc.tile_pool(name="scratch", bufs=4))
+        results = ctx.enter_context(tc.tile_pool(name="results", bufs=3))
+        turned = ctx.enter_context(tc.psum_pool(name="turned", bufs=2))
+        sums = ctx.enter_context(tc.psum_pool(name="sums", bufs=2))
+        back = ctx.enter_context(tc.psum_pool(name="back", bufs=3))
+        plain = ctx.enter_context(tc.psum_pool(name="plain", bufs=1))
+        ctx.enter_context(tc.manual_schedule())
+
         x_sb = keep.tile([P, TILES, HID], BF16)
-        w_raw = keep.tile([P, PASSES, 2 * COLS], U8)
         w_words = keep.tile([P, PASSES, 2 * COLS], U8, align_bytes=64)
-        scale_raw = keep.tile([P, PASSES, COLS], U8)
         w_scales = keep.tile([P, PASSES, COLS], U8, align_bytes=64)
+        nope_words = keep.tile([P, PASSES, 2 * HEADS * NOPE], U8, align_bytes=64)
+        nope_scales = keep.tile([P, PASSES, HEADS * NOPE], U8, align_bytes=64)
         bias_row = keep.tile([P, COLS], BF16)
         ones = keep.tile([P, P], BF16)
-        bias = keep.tile([P, COLS], F32)
+        bias_nope = keep.tile([P, HEADS, NOPE], F32)
+        bias_col = keep.tile([P, HEADS], F32)
         angles = keep.tile([P, 2, TILES, ROPE], BF16)
         identity = keep.tile([P, P], F32)
-        identity_bf = keep.tile([P, P], BF16)
+        codes = []
+        code_scales = []
+        for j in range(BLOCKS):
+            block_codes = keep.tile([P, PASSES, BLOCK * P], U32, align_bytes=64, name="codes%d" % j)
+            block_scales = keep.tile([P, PASSES, BLOCK * P], U8, align_bytes=64, name="code_scales%d" % j)
+            codes.append(block_codes)
+            code_scales.append(block_scales)
 
         nc.vector.memset(bias_row[:].bitcast(I32), 0)
-        nc.vector.memset(scale_raw[:].bitcast(I32), 0)
+        nc.vector.memset(w_scales[:].bitcast(I32), 0)
         nc.vector.memset(ones[:], 1.0)
         make_identity(nc, identity[:])
-        make_identity(nc, identity_bf[:])
 
         def load_x(tiles):
             nc.sync.dma_start(out=x_sb[:, tiles, :], in_=x_dram[:, tiles, :])
@@ -87,144 +85,197 @@ def tile_gptossmlaattention_pb_kernel(tc, hidden_states, cos, sin, Wq_words, Wq_
             nc.sync.dma_start(out=angles[:, 0, tiles, :], in_=cos_dram[:, tiles, :])
             nc.sync.dma_start(out=angles[:, 1, tiles, :], in_=sin_dram[:, tiles, :])
 
-        early = slice(0, 4)
-        late = slice(4, TILES)
+        early = slice(0, BLOCK)
+        late = slice(BLOCK, TILES)
         load_x(slice(0, 1))
         nc.sync.dma_start(out=bias_row[0:1, :], in_=bq.unsqueeze(0))
         for r in range(4):
             nc.sync.dma_start(
-                out=scale_raw[r:P:32].bitcast(I32),
+                out=w_scales[r:P:32].bitcast(I32),
                 in_=Wq_scales[:, r:16:4, :].rearrange("g q n -> q g n").bitcast(I32),
             )
-        nc.sync.dma_start(out=w_raw[:].bitcast(I32), in_=Wq_words.rearrange("g p n -> p g n").bitcast(I32))
+        nc.sync.dma_start(out=w_words[:].bitcast(I32), in_=Wq_words.rearrange("g p n -> p g n").bitcast(I32))
         load_x(slice(1, 2))
+        load_x(slice(2, 3))
+        load_x(slice(3, 4))
         load_angles(early)
-        load_x(slice(2, 4))
+        load_x(slice(4, 6))
+        load_x(slice(6, 8))
         load_angles(late)
-        for first in range(4, TILES, 2):
+        for first in range(8, TILES, 2):
             load_x(slice(first, first + 2))
 
-        bias_by_head = bias[:].rearrange("p (h d) -> p h d", h=HEADS)
+        def turn(first, count):
+            grouped = staging.tile([P, PASSES, count * P * 4], BF16, align_bytes=64, name="grouped")
+            grouped_words = grouped[:].bitcast(F32)
+            for i in range(count):
+                x_words = x_sb[:, first + i, :].bitcast(F32)
+                flipped = turned.tile([P, 2 * PASSES, P], F32, name="flipped")
+                for g in range(PASSES):
+                    for u in range(2):
+                        start = g * (K_PASS // 2) + u
+                        nc.tensor.transpose(flipped[:, 2 * g + u, :], x_words[:, start : (g + 1) * (K_PASS // 2) : 2], identity[:])
+                nc.scalar.copy(
+                    out=grouped_words[:, :, i * 2 * P : (i + 1) * 2 * P].rearrange("p g (r u) -> p g r u", u=2),
+                    in_=flipped[:].rearrange("p (g u) r -> p g r u", u=2),
+                )
+            return grouped
 
-        def new_banks():
-            banks = []
-            for b in range(BANKS):
-                bank = sums.tile([P, BANK], F32, name="bank%d" % b)
-                banks.append(bank)
-            return banks
+        def quantise(grouped, first, count):
+            j, i = divmod(first, BLOCK)
+            columns = slice(i * P, (i + count) * P)
+            for g in range(PASSES):
+                nc.vector.quantize_mx(
+                    out=codes[j][:, g, columns].bitcast(FP8X4), scales=code_scales[j][:, g, columns], in_=grouped[:, g, :]
+                )
 
-        def spread_bias():
-            banks = new_banks()
-            for b in range(BANKS):
-                columns = slice(b * BANK, (b + 1) * BANK)
-                nc.tensor.matmul(out=banks[b][:], lhsT=ones[:], rhs=bias_row[:, columns], start=True, stop=True)
-                nc.scalar.copy(out=bias[:, columns], in_=banks[b][:])
+        def multiply_unrotated(t):
+            j, i = divmod(t, BLOCK)
+            columns = slice(i * P, (i + 1) * P)
+            bank = plain.tile([P, HEADS, NOPE], F32, name="unrotated")
+            for g in range(PASSES):
+                nc.tensor.matmul_mx(
+                    out=bank[:].rearrange("p h d -> p (h d)"),
+                    lhsT=codes[j][:, g, columns].bitcast(FP8X4),
+                    lhsT_scale=code_scales[j][:, g, columns],
+                    rhs=nope_words[:, g, :].bitcast(FP4X4),
+                    rhs_scale=nope_scales[:, g, :],
+                    start=(g == 0),
+                    stop=(g == PASSES - 1),
+                )
+            return bank
+
+        def multiply_rotated(j, h):
+            first = h * HEAD + NOPE
+            bank = sums.tile([P, BLOCK * P], F32, name="by_channel_sums")
+            for g in range(PASSES):
+                nc.tensor.matmul_mx(
+                    out=bank[:],
+                    lhsT=w_words[:, g, 2 * first : 2 * (first + ROPE)].bitcast(FP4X4),
+                    lhsT_scale=w_scales[:, g, first : first + ROPE],
+                    rhs=codes[j][:, g, :].bitcast(FP8X4),
+                    rhs_scale=code_scales[j][:, g, :],
+                    start=(g == 0),
+                    stop=(g == PASSES - 1),
+                )
+            return bank
+
+        def add_bias(h, bank):
+            by_channel = channels.tile([P, BLOCK * P], F32, name="by_channel")
+            nc.scalar.activation(out=by_channel[:], in_=bank[:], func=IDENTITY, bias=bias_col[:, h : h + 1], scale=1.0)
+            return by_channel
+
+        def turn_back(by_channel):
+            upright = back.tile([P, BLOCK, ROPE], F32, name="upright")
+            for i in range(BLOCK):
+                nc.tensor.transpose(upright[:, i, :], by_channel[:, i * P : (i + 1) * P], identity[:])
+            return upright
+
+        def rotate(j, h, upright, result):
+            tiles = slice(j * BLOCK, (j + 1) * BLOCK)
+            rotated = result[:, h, :, NOPE:HEAD]
+            nc.vector.tensor_tensor(out=rotated, in0=upright[:], in1=angles[:, 0, tiles, :], op=MULT)
+            crossed = scratch.tile([P, BLOCK, ROPE], F32, name="crossed")
+            for f in range(2):
+                here = slice(f * HALF, (f + 1) * HALF)
+                there = slice((1 - f) * HALF, (2 - f) * HALF)
+                nc.vector.tensor_tensor(out=crossed[:, :, here], in0=upright[:, :, there], in1=angles[:, 1, tiles, here], op=MULT)
+            nc.gpsimd.tensor_tensor(out=rotated, in0=rotated, in1=crossed[:], op=ADD)
 
         def negate_first_half_of_sin(tiles):
             nc.scalar.mul(out=angles[:, 1, tiles, 0:HALF], in_=angles[:, 1, tiles, 0:HALF], mul=-1.0)
 
-        def angles_to_psum(t):
-            table = tables.tile([P, 2, ROPE], F32)
-            nc.tensor.matmul(out=table[:], lhsT=identity_bf[:], rhs=angles[:, :, t, :], start=True, stop=True)
-            return table
+        def store(j, heads, result):
+            nc.sync.dma_start(out=out_dram[:, heads, j * BLOCK : (j + 1) * BLOCK, :], in_=result[:, heads, :, :])
 
-        def turn_tile(t):
-            x_words = x_sb[:, t, :].bitcast(F32)
-            flipped = turned.tile([P, 2 * PASSES, P], F32)
-            for g in range(PASSES):
-                for u in range(2):
-                    first = g * (K_PASS // 2) + u
-                    nc.tensor.transpose(flipped[:, 2 * g + u, :], x_words[:, first : (g + 1) * (K_PASS // 2) : 2], identity[:])
-            grouped = words.tile([P, PASSES * P * 4], BF16, align_bytes=64)
-            nc.scalar.copy(
-                out=grouped[:].bitcast(F32).rearrange("p (g r u) -> p g r u", g=PASSES, u=2),
-                in_=flipped[:].rearrange("p (g u) r -> p g r u", u=2),
-            )
-            return grouped
+        result_of = {}
 
-        def quantise_tile(grouped):
-            codes = words.tile([P, PASSES * P], U32, align_bytes=64)
-            code_scales = words.tile([P, PASSES * P], U8, align_bytes=64)
-            nc.vector.quantize_mx(out=codes[:].bitcast(FP8X4), scales=code_scales[:], in_=grouped[:])
-            return codes, code_scales
+        def result_for(j):
+            if j not in result_of:
+                result = results.tile([P, HEADS, BLOCK, HEAD], F32, name="result")
+                result_of[j] = result
+            return result_of[j]
 
-        def multiply_tile(codes, code_scales):
-            banks = new_banks()
-            for b in range(BANKS):
-                for g in range(PASSES):
-                    nc.tensor.matmul_mx(
-                        out=banks[b][:],
-                        lhsT=codes[:, g * P : (g + 1) * P].bitcast(FP8X4),
-                        lhsT_scale=code_scales[:, g * P : (g + 1) * P],
-                        rhs=w_words[:, g, 2 * b * BANK : 2 * (b + 1) * BANK].bitcast(FP4X4),
-                        rhs_scale=w_scales[:, g, b * BANK : (b + 1) * BANK],
-                        start=(g == 0),
-                        stop=(g == PASSES - 1),
-                    )
-            return banks
+        def on_vector(t):
+            return t % 2 == 0
 
-        def finish_tile(banks, table, result):
-            nc.scalar.copy(out=result[:, :, 0:NOPE], in_=banks[ROPE_BANKS][:].rearrange("p (h d) -> p h d", h=HEADS))
-            nc.gpsimd.tensor_tensor(
-                out=result[:, :, 0:NOPE], in0=result[:, :, 0:NOPE], in1=bias_by_head[:, :, 0:NOPE], op=ADD
-            )
-            x = scratch.tile([P, HEADS, ROPE], F32)
-            for b in range(ROPE_BANKS):
-                heads = slice(b * HEADS_PER_BANK, (b + 1) * HEADS_PER_BANK)
-                nc.vector.tensor_tensor(
-                    out=x[:, heads, :],
-                    in0=banks[b][:].rearrange("p (h d) -> p h d", h=HEADS_PER_BANK),
-                    in1=bias_by_head[:, heads, NOPE:HEAD],
-                    op=ADD,
-                )
-            nc.vector.tensor_tensor(
-                out=result[:, :, NOPE:HEAD],
-                in0=x[:],
-                in1=table[:, 0, :].unsqueeze(1).to_broadcast([P, HEADS, ROPE]),
-                op=MULT,
-            )
-            crossed = scratch.tile([P, HEADS, ROPE], F32)
-            for f in range(2):
-                here = slice(f * HALF, (f + 1) * HALF)
-                there = slice((1 - f) * HALF, (2 - f) * HALF)
-                nc.vector.tensor_tensor(
-                    out=crossed[:, :, here],
-                    in0=x[:, :, there],
-                    in1=table[:, 1, here].unsqueeze(1).to_broadcast([P, HEADS, HALF]),
-                    op=MULT,
-                )
-            nc.gpsimd.tensor_tensor(out=result[:, :, NOPE:HEAD], in0=result[:, :, NOPE:HEAD], in1=crossed[:], op=ADD)
+        def copy_unrotated(t, bank):
+            place = result_for(t // BLOCK)[:, :, t % BLOCK, 0:NOPE]
+            nc.scalar.copy(out=place, in_=bank[:])
 
-        def store_tile(t, result):
-            place = t % TILES_PER_STORE
-            if t >= TILES - TILES_PER_STORE:
-                nc.sync.dma_start(out=out_dram[:, :, t, :], in_=result[:, :, place, :])
-            elif place == TILES_PER_STORE - 1:
-                nc.sync.dma_start(out=out_dram[:, :, t + 1 - TILES_PER_STORE : t + 1, :], in_=result[:])
+        def bias_unrotated(t, bank):
+            place = result_for(t // BLOCK)[:, :, t % BLOCK, 0:NOPE]
+            if on_vector(t):
+                nc.vector.tensor_tensor(out=place, in0=bank[:], in1=bias_nope[:], op=ADD)
+            else:
+                nc.gpsimd.tensor_tensor(out=place, in0=place, in1=bias_nope[:], op=ADD)
 
-        quantised = {}
-        banks = {}
-        quantised[0] = quantise_tile(turn_tile(0))
-        spread_bias()
-        sort_columns(nc, w_scales[:], scale_raw[:], 1)
-        sort_columns(nc, w_words[:], w_raw[:], 2)
-        quantised[1] = quantise_tile(turn_tile(1))
+        quantise(turn(0, 1), 0, 1)
+        spread = plain.tile([P, HEADS, NOPE], F32, name="unrotated")
+        nc.tensor.matmul(
+            out=spread[:].rearrange("p h d -> p (h d)"),
+            lhsT=ones[:],
+            rhs=bias_row[:].rearrange("p (h c) -> p h c", h=HEADS)[:, :, 0:NOPE],
+            start=True,
+            stop=True,
+        )
+        nc.scalar.copy(out=bias_nope[:], in_=spread[:])
+        stood = back.tile([P, HEADS], F32, name="upright")
+        for h in range(HEADS):
+            first = h * HEAD + NOPE
+            nc.tensor.matmul(out=stood[:, h : h + 1], lhsT=bias_row[:, first : first + ROPE], rhs=ones[:, 0:1], start=True, stop=True)
+        nc.scalar.copy(out=bias_col[:], in_=stood[:])
+        nc.vector.tensor_copy(
+            out=nope_scales[:].bitcast(I32).rearrange("p g (h c) -> p g h c", h=HEADS),
+            in_=w_scales[:].bitcast(I32).rearrange("p g (h c) -> p g h c", h=HEADS)[:, :, :, 0 : NOPE // 4],
+        )
+        nc.vector.tensor_copy(
+            out=nope_words[:].bitcast(I32).rearrange("p g (h c) -> p g h c", h=HEADS),
+            in_=w_words[:].bitcast(I32).rearrange("p g (h c) -> p g h c", h=HEADS)[:, :, :, 0 : NOPE // 2],
+        )
+        for t in range(1, BLOCK):
+            quantise(turn(t, 1), t, 1)
+            if t - 1 < NOPE_LEAD:
+                bank = multiply_unrotated(t - 1)
+                if not on_vector(t - 1):
+                    copy_unrotated(t - 1, bank)
+                bias_unrotated(t - 1, bank)
         negate_first_half_of_sin(early)
-        banks[0] = multiply_tile(*quantised[0])
 
-        result = None
-        for t in range(TILES):
-            table = angles_to_psum(t)
-            grouped = None
-            if t + 2 < TILES:
-                grouped = turn_tile(t + 2)
-            if t + 1 < TILES:
-                banks[t + 1] = multiply_tile(*quantised[t + 1])
-            if t % TILES_PER_STORE == 0:
-                result = results.tile([P, HEADS, TILES_PER_STORE, HEAD], F32)
-            finish_tile(banks[t], table, result[:, :, t % TILES_PER_STORE, :])
-            store_tile(t, result)
-            if t + 2 < TILES:
-                quantised[t + 2] = quantise_tile(grouped)
-            if t == 0:
+        for slot in range(SLOTS):
+            j, q = divmod(slot, SLOTS_PER_BLOCK)
+            heads = (2 * q, 2 * q + 1)
+            result = result_for(j)
+            banks = {}
+            for h in heads:
+                banks[h] = multiply_rotated(j, h)
+            t = slot + NOPE_LEAD
+            unrotated = None
+            if t < TILES:
+                unrotated = multiply_unrotated(t)
+            by_channel = {}
+            for h in heads:
+                by_channel[h] = add_bias(h, banks[h])
+            if t < TILES and not on_vector(t):
+                copy_unrotated(t, unrotated)
+            upright = {}
+            for h in heads:
+                upright[h] = turn_back(by_channel[h])
+            fresh = []
+            for k in range(BLOCK // 2, TILES // 2):
+                if max(k - 2, 2 * k - 5) == slot:
+                    fresh.append((turn(2 * k, 2), 2 * k))
+            if t < TILES:
+                bias_unrotated(t, unrotated)
+            for h in heads:
+                rotate(j, h, upright[h], result)
+                if j == BLOCKS - 1 and q == SLOTS_PER_BLOCK - 1:
+                    store(j, slice(h, h + 1), result)
+            for grouped, first in fresh:
+                quantise(grouped, first, 2)
+            if slot == 1:
                 negate_first_half_of_sin(late)
+            if q == 1:
+                store(j, slice(0, 4), result)
+            elif q == 2 or (q == 3 and j < BLOCKS - 1):
+                store(j, slice(2 * q, 2 * q + 2), result)

@@ -30,7 +30,6 @@ BLOCK = 4
 BLOCKS = TILES // BLOCK
 SLOTS_PER_BLOCK = HEADS // 2
 SLOTS = BLOCKS * SLOTS_PER_BLOCK
-NOPE_LEAD = 2
 
 FLOPS = 2 * SEQ * HID * COLS
 
@@ -48,10 +47,9 @@ def tile_gptossmlaattention_pb_kernel(tc, hidden_states, cos, sin, Wq_words, Wq_
         channels = ctx.enter_context(tc.tile_pool(name="channels", bufs=4))
         scratch = ctx.enter_context(tc.tile_pool(name="scratch", bufs=4))
         results = ctx.enter_context(tc.tile_pool(name="results", bufs=3))
-        turned = ctx.enter_context(tc.psum_pool(name="turned", bufs=2))
+        short = ctx.enter_context(tc.psum_pool(name="short", bufs=3))
         sums = ctx.enter_context(tc.psum_pool(name="sums", bufs=2))
         back = ctx.enter_context(tc.psum_pool(name="back", bufs=3))
-        plain = ctx.enter_context(tc.psum_pool(name="plain", bufs=1))
         ctx.enter_context(tc.manual_schedule())
 
         x_sb = keep.tile([P, TILES, HID], BF16)
@@ -87,17 +85,19 @@ def tile_gptossmlaattention_pb_kernel(tc, hidden_states, cos, sin, Wq_words, Wq_
 
         early = slice(0, BLOCK)
         late = slice(BLOCK, TILES)
-        load_x(slice(0, 1))
+        for t in range(BLOCK):
+            load_x(slice(t, t + 1))
         nc.sync.dma_start(out=bias_row[0:1, :], in_=bq.unsqueeze(0))
         for r in range(4):
             nc.sync.dma_start(
                 out=w_scales[r:P:32].bitcast(I32),
                 in_=Wq_scales[:, r:16:4, :].rearrange("g q n -> q g n").bitcast(I32),
             )
-        nc.sync.dma_start(out=w_words[:].bitcast(I32), in_=Wq_words.rearrange("g p n -> p g n").bitcast(I32))
-        load_x(slice(1, 2))
-        load_x(slice(2, 3))
-        load_x(slice(3, 4))
+        half_words = 2 * COLS // 8
+        w_sbuf = w_words[:].bitcast(I32)
+        w_dram = Wq_words.rearrange("g p n -> p g n").bitcast(I32)
+        nc.sync.dma_start(out=w_sbuf[:, :, 0:half_words], in_=w_dram[:, :, 0:half_words])
+        nc.sync.dma_start(out=w_sbuf[:, :, half_words:], in_=w_dram[:, :, half_words:])
         load_angles(early)
         load_x(slice(4, 6))
         load_x(slice(6, 8))
@@ -110,7 +110,7 @@ def tile_gptossmlaattention_pb_kernel(tc, hidden_states, cos, sin, Wq_words, Wq_
             grouped_words = grouped[:].bitcast(F32)
             for i in range(count):
                 x_words = x_sb[:, first + i, :].bitcast(F32)
-                flipped = turned.tile([P, 2 * PASSES, P], F32, name="flipped")
+                flipped = short.tile([P, 2 * PASSES, P], F32, name="brief")
                 for g in range(PASSES):
                     for u in range(2):
                         start = g * (K_PASS // 2) + u
@@ -132,7 +132,7 @@ def tile_gptossmlaattention_pb_kernel(tc, hidden_states, cos, sin, Wq_words, Wq_
         def multiply_unrotated(t):
             j, i = divmod(t, BLOCK)
             columns = slice(i * P, (i + 1) * P)
-            bank = plain.tile([P, HEADS, NOPE], F32, name="unrotated")
+            bank = short.tile([P, HEADS, NOPE], F32, name="brief")
             for g in range(PASSES):
                 nc.tensor.matmul_mx(
                     out=bank[:].rearrange("p h d -> p (h d)"),
@@ -210,8 +210,9 @@ def tile_gptossmlaattention_pb_kernel(tc, hidden_states, cos, sin, Wq_words, Wq_
             else:
                 nc.gpsimd.tensor_tensor(out=place, in0=place, in1=bias_nope[:], op=ADD)
 
-        quantise(turn(0, 1), 0, 1)
-        spread = plain.tile([P, HEADS, NOPE], F32, name="unrotated")
+        for t in range(BLOCK):
+            quantise(turn(t, 1), t, 1)
+        spread = short.tile([P, HEADS, NOPE], F32, name="brief")
         nc.tensor.matmul(
             out=spread[:].rearrange("p h d -> p (h d)"),
             lhsT=ones[:],
@@ -233,15 +234,23 @@ def tile_gptossmlaattention_pb_kernel(tc, hidden_states, cos, sin, Wq_words, Wq_
             out=nope_words[:].bitcast(I32).rearrange("p g (h c) -> p g h c", h=HEADS),
             in_=w_words[:].bitcast(I32).rearrange("p g (h c) -> p g h c", h=HEADS)[:, :, :, 0 : NOPE // 2],
         )
-        for t in range(1, BLOCK):
-            quantise(turn(t, 1), t, 1)
-            if t - 1 < NOPE_LEAD:
-                bank = multiply_unrotated(t - 1)
-                if not on_vector(t - 1):
-                    copy_unrotated(t - 1, bank)
-                bias_unrotated(t - 1, bank)
-        negate_first_half_of_sin(early)
 
+        def turn_slot(k):
+            return max(k - 2, 2 * k - 5)
+
+        all_turned = turn_slot(TILES // 2 - 1) + 1
+
+        def unrotated_tiles(slot):
+            if slot < all_turned:
+                return [slot]
+            if slot < all_turned + 2:
+                return [2 * slot - all_turned, 2 * slot - all_turned + 1]
+            if slot + 2 < TILES:
+                return [slot + 2]
+            return []
+
+        unstored = []
+        done_tiles = 0
         for slot in range(SLOTS):
             j, q = divmod(slot, SLOTS_PER_BLOCK)
             heads = (2 * q, 2 * q + 1)
@@ -249,33 +258,46 @@ def tile_gptossmlaattention_pb_kernel(tc, hidden_states, cos, sin, Wq_words, Wq_
             banks = {}
             for h in heads:
                 banks[h] = multiply_rotated(j, h)
-            t = slot + NOPE_LEAD
-            unrotated = None
-            if t < TILES:
-                unrotated = multiply_unrotated(t)
+            unrotated = {}
+            for t in unrotated_tiles(slot):
+                unrotated[t] = multiply_unrotated(t)
             by_channel = {}
             for h in heads:
                 by_channel[h] = add_bias(h, banks[h])
-            if t < TILES and not on_vector(t):
-                copy_unrotated(t, unrotated)
-            upright = {}
-            for h in heads:
-                upright[h] = turn_back(by_channel[h])
+            if slot == 0:
+                negate_first_half_of_sin(early)
+            for t in unrotated_tiles(slot):
+                if not on_vector(t):
+                    copy_unrotated(t, unrotated[t])
             fresh = []
+            upright = {}
+            if slot == 0:
+                for h in heads:
+                    upright[h] = turn_back(by_channel[h])
             for k in range(BLOCK // 2, TILES // 2):
-                if max(k - 2, 2 * k - 5) == slot:
+                if turn_slot(k) == slot:
                     fresh.append((turn(2 * k, 2), 2 * k))
-            if t < TILES:
-                bias_unrotated(t, unrotated)
+            if slot > 0:
+                for h in heads:
+                    upright[h] = turn_back(by_channel[h])
+            for t in unrotated_tiles(slot):
+                bias_unrotated(t, unrotated[t])
+                done_tiles = t + 1
+            last = slot == SLOTS - 1
             for h in heads:
                 rotate(j, h, upright[h], result)
-                if j == BLOCKS - 1 and q == SLOTS_PER_BLOCK - 1:
+                if last:
                     store(j, slice(h, h + 1), result)
             for grouped, first in fresh:
                 quantise(grouped, first, 2)
             if slot == 1:
                 negate_first_half_of_sin(late)
-            if q == 1:
-                store(j, slice(0, 4), result)
-            elif q == 2 or (q == 3 and j < BLOCKS - 1):
-                store(j, slice(2 * q, 2 * q + 2), result)
+            if not last:
+                unstored.append((j, 2 * q))
+            held = []
+            for block, first in unstored:
+                if done_tiles >= (block + 1) * BLOCK:
+                    store(block, slice(first, first + 2), result_of[block])
+                else:
+                    held.append((block, first))
+            unstored = held

@@ -45,7 +45,7 @@ def tile_gptossmlaattention_pb_kernel(tc, hidden_states, cos, sin, Wq_words, Wq_
         keep = ctx.enter_context(tc.tile_pool(name="keep", bufs=1))
         staging = ctx.enter_context(tc.tile_pool(name="staging", bufs=3))
         channels = ctx.enter_context(tc.tile_pool(name="channels", bufs=4))
-        scratch = ctx.enter_context(tc.tile_pool(name="scratch", bufs=4))
+        scratch = ctx.enter_context(tc.tile_pool(name="scratch", bufs=3))
         results = ctx.enter_context(tc.tile_pool(name="results", bufs=3))
         short = ctx.enter_context(tc.psum_pool(name="short", bufs=3))
         sums = ctx.enter_context(tc.psum_pool(name="sums", bufs=2))
@@ -171,15 +171,18 @@ def tile_gptossmlaattention_pb_kernel(tc, hidden_states, cos, sin, Wq_words, Wq_
                 nc.tensor.transpose(upright[:, i, :], by_channel[:, i * P : (i + 1) * P], identity[:])
             return upright
 
-        def rotate(j, h, upright, result):
+        def rotate(j, heads, upright, result):
             tiles = slice(j * BLOCK, (j + 1) * BLOCK)
-            rotated = result[:, h, :, NOPE:HEAD]
-            nc.vector.tensor_tensor(out=rotated, in0=upright[:], in1=angles[:, 0, tiles, :], op=MULT)
-            crossed = scratch.tile([P, BLOCK, ROPE], F32, name="crossed")
-            for f in range(2):
-                here = slice(f * HALF, (f + 1) * HALF)
-                there = slice((1 - f) * HALF, (2 - f) * HALF)
-                nc.vector.tensor_tensor(out=crossed[:, :, here], in0=upright[:, :, there], in1=angles[:, 1, tiles, here], op=MULT)
+            crossed = scratch.tile([P, len(heads), BLOCK, ROPE], F32, name="crossed")
+            for n in range(len(heads)):
+                nc.vector.tensor_tensor(out=result[:, heads[n], :, NOPE:HEAD], in0=upright[heads[n]][:], in1=angles[:, 0, tiles, :], op=MULT)
+                nc.vector.tensor_tensor(
+                    out=crossed[:, n, :, :].rearrange("p i (f d) -> p i f d", f=2),
+                    in0=upright[heads[n]][:].rearrange("p i (f d) -> p i f d", f=2)[:, :, ::-1, :],
+                    in1=angles[:, 1, tiles, :].rearrange("p i (f d) -> p i f d", f=2),
+                    op=MULT,
+                )
+            rotated = result[:, heads[0] : heads[0] + len(heads), :, NOPE:HEAD]
             nc.gpsimd.tensor_tensor(out=rotated, in0=rotated, in1=crossed[:], op=ADD)
 
         def negate_first_half_of_sin(tiles):
@@ -284,10 +287,12 @@ def tile_gptossmlaattention_pb_kernel(tc, hidden_states, cos, sin, Wq_words, Wq_
                 bias_unrotated(t, unrotated[t])
                 done_tiles = t + 1
             last = slot == SLOTS - 1
-            for h in heads:
-                rotate(j, h, upright[h], result)
-                if last:
+            if last:
+                for h in heads:
+                    rotate(j, (h,), upright, result)
                     store(j, slice(h, h + 1), result)
+            else:
+                rotate(j, heads, upright, result)
             for grouped, first in fresh:
                 quantise(grouped, first, 2)
             if slot == 1:

@@ -62,6 +62,7 @@ def tile_gptossmlaattention_pb_kernel(tc, hidden_states, cos, sin, Wq_words, Wq_
         bias_nope = keep.tile([P, HEADS, NOPE], F32)
         bias_col = keep.tile([P, HEADS], F32)
         angles = keep.tile([P, 2, TILES, ROPE], BF16)
+        sin_raw = keep.tile([P, TILES, ROPE], BF16)
         identity = keep.tile([P, P], F32)
         codes = []
         code_scales = []
@@ -81,7 +82,7 @@ def tile_gptossmlaattention_pb_kernel(tc, hidden_states, cos, sin, Wq_words, Wq_
 
         def load_angles(tiles):
             nc.sync.dma_start(out=angles[:, 0, tiles, :], in_=cos_dram[:, tiles, :])
-            nc.sync.dma_start(out=angles[:, 1, tiles, :], in_=sin_dram[:, tiles, :])
+            nc.sync.dma_start(out=sin_raw[:, tiles, :], in_=sin_dram[:, tiles, :])
 
         early = slice(0, BLOCK)
         late = slice(BLOCK, TILES)
@@ -173,20 +174,25 @@ def tile_gptossmlaattention_pb_kernel(tc, hidden_states, cos, sin, Wq_words, Wq_
 
         def rotate(j, heads, upright, result):
             tiles = slice(j * BLOCK, (j + 1) * BLOCK)
-            crossed = scratch.tile([P, len(heads), BLOCK, ROPE], F32, name="crossed")
-            for n in range(len(heads)):
-                nc.vector.tensor_tensor(out=result[:, heads[n], :, NOPE:HEAD], in0=upright[heads[n]][:], in1=angles[:, 0, tiles, :], op=MULT)
+            count = len(heads)
+            products = scratch.tile([P, 2, count, BLOCK, ROPE], F32, name="products")
+            for n in range(count):
                 nc.vector.tensor_tensor(
-                    out=crossed[:, n, :, :].rearrange("p i (f d) -> p i f d", f=2),
-                    in0=upright[heads[n]][:].rearrange("p i (f d) -> p i f d", f=2)[:, :, ::-1, :],
-                    in1=angles[:, 1, tiles, :].rearrange("p i (f d) -> p i f d", f=2),
+                    out=products[:, :, n, :, :].rearrange("p r i d -> p r (i d)"),
+                    in0=upright[heads[n]][:].rearrange("p i d -> p (i d)").unsqueeze(1).to_broadcast([P, 2, BLOCK * ROPE]),
+                    in1=angles[:, :, tiles, :].rearrange("p r i d -> p r (i d)"),
                     op=MULT,
                 )
-            rotated = result[:, heads[0] : heads[0] + len(heads), :, NOPE:HEAD]
-            nc.gpsimd.tensor_tensor(out=rotated, in0=rotated, in1=crossed[:], op=ADD)
+            nc.gpsimd.tensor_tensor(
+                out=result[:, heads[0] : heads[0] + count, :, NOPE:HEAD].rearrange("p n i (f d) -> p (n i) f d", f=2),
+                in0=products[:, 0, :, :, :].rearrange("p n i (f d) -> p (n i) f d", f=2),
+                in1=products[:, 1, :, :, :].rearrange("p n i (f d) -> p (n i) f d", f=2)[:, :, ::-1, :],
+                op=ADD,
+            )
 
         def negate_first_half_of_sin(tiles):
-            nc.scalar.mul(out=angles[:, 1, tiles, 0:HALF], in_=angles[:, 1, tiles, 0:HALF], mul=-1.0)
+            nc.scalar.copy(out=angles[:, 1, tiles, 0:HALF], in_=sin_raw[:, tiles, HALF:ROPE])
+            nc.scalar.mul(out=angles[:, 1, tiles, HALF:ROPE], in_=sin_raw[:, tiles, 0:HALF], mul=-1.0)
 
         def store(j, heads, result):
             nc.sync.dma_start(out=out_dram[:, heads, j * BLOCK : (j + 1) * BLOCK, :], in_=result[:, heads, :, :])

@@ -206,7 +206,7 @@ def tile_gptossmlaattention_pb_kernel(tc, hidden_states, cos, sin, Wq_words, Wq_
             return result_of[j]
 
         def on_vector(t):
-            return t % 2 == 0
+            return t % BLOCK != 0
 
         def copy_unrotated(t, bank):
             place = result_for(t // BLOCK)[:, :, t % BLOCK, 0:NOPE]

@@ -172,7 +172,7 @@ def tile_gptossmlaattention_pb_kernel(tc, hidden_states, cos, sin, Wq_words, Wq_
                 nc.tensor.transpose(upright[:, i, :], by_channel[:, i * P : (i + 1) * P], identity[:])
             return upright
 
-        def rotate(j, heads, upright, result):
+        def rotate(j, heads, upright, result, adder):
             tiles = slice(j * BLOCK, (j + 1) * BLOCK)
             count = len(heads)
             products = scratch.tile([P, 2, count, BLOCK, ROPE], F32, name="products")
@@ -183,7 +183,7 @@ def tile_gptossmlaattention_pb_kernel(tc, hidden_states, cos, sin, Wq_words, Wq_
                     in1=angles[:, :, tiles, :].rearrange("p r i d -> p r (i d)"),
                     op=MULT,
                 )
-            nc.gpsimd.tensor_tensor(
+            adder.tensor_tensor(
                 out=result[:, heads[0] : heads[0] + count, :, NOPE:HEAD].rearrange("p n i (f d) -> p (n i) f d", f=2),
                 in0=products[:, 0, :, :, :].rearrange("p n i (f d) -> p (n i) f d", f=2),
                 in1=products[:, 1, :, :, :].rearrange("p n i (f d) -> p (n i) f d", f=2)[:, :, ::-1, :],
@@ -247,68 +247,74 @@ def tile_gptossmlaattention_pb_kernel(tc, hidden_states, cos, sin, Wq_words, Wq_
         def turn_slot(k):
             return max(k - 2, 2 * k - 5)
 
-        all_turned = turn_slot(TILES // 2 - 1) + 1
+        turning_steps = []
+        for k in range(BLOCK // 2, TILES // 2):
+            turning_steps.append(turn_slot(k))
+        free_steps = []
+        for s in range(SLOTS):
+            if s not in turning_steps:
+                free_steps.append(s)
 
-        def unrotated_tiles(slot):
-            if slot < all_turned:
-                return [slot]
-            if slot < all_turned + 2:
-                return [2 * slot - all_turned, 2 * slot - all_turned + 1]
-            if slot + 2 < TILES:
-                return [slot + 2]
+        def unrotated_tiles(step):
+            if step in free_steps and 2 * free_steps.index(step) < TILES:
+                return [2 * free_steps.index(step), 2 * free_steps.index(step) + 1]
             return []
 
+        units = []
+        for j in range(BLOCKS):
+            for h in range(HEADS):
+                units.append((j, h))
+        by_channel = {}
         unstored = []
         done_tiles = 0
-        for slot in range(SLOTS):
-            j, q = divmod(slot, SLOTS_PER_BLOCK)
-            heads = (2 * q, 2 * q + 1)
-            result = result_for(j)
+        for step in range(SLOTS + 1):
+            fresh = [n for n in (2 * step, 2 * step + 1) if n < len(units)]
+            ripe = [n for n in (2 * step - 1, 2 * step) if 0 <= n < len(units)]
+            flat = unrotated_tiles(step)
             banks = {}
-            for h in heads:
-                banks[h] = multiply_rotated(j, h)
+            for n in fresh:
+                banks[n] = multiply_rotated(units[n][0], units[n][1])
             unrotated = {}
-            for t in unrotated_tiles(slot):
+            for t in flat:
                 unrotated[t] = multiply_unrotated(t)
-            by_channel = {}
-            for h in heads:
-                by_channel[h] = add_bias(h, banks[h])
-            if slot == 0:
+            for n in fresh:
+                by_channel[n] = add_bias(units[n][1], banks[n])
+            if step == 0:
                 negate_first_half_of_sin(early)
-            for t in unrotated_tiles(slot):
+            for t in flat:
                 if not on_vector(t):
                     copy_unrotated(t, unrotated[t])
-            fresh = []
             upright = {}
-            if slot == 0:
-                for h in heads:
-                    upright[h] = turn_back(by_channel[h])
-            for k in range(BLOCK // 2, TILES // 2):
-                if turn_slot(k) == slot:
-                    fresh.append((turn(2 * k, 2), 2 * k))
-            if slot > 0:
-                for h in heads:
-                    upright[h] = turn_back(by_channel[h])
-            for t in unrotated_tiles(slot):
+            turned_now = []
+            for n in ripe:
+                if n == 2 * step and step > 0:
+                    for k in range(BLOCK // 2, TILES // 2):
+                        if turn_slot(k) == step:
+                            turned_now.append((turn(2 * k, 2), 2 * k))
+                upright[units[n][1]] = turn_back(by_channel[n])
+            if step == 0:
+                turned_now.append((turn(BLOCK, 2), BLOCK))
+            for t in flat:
                 bias_unrotated(t, unrotated[t])
                 done_tiles = t + 1
-            last = slot == SLOTS - 1
-            if last:
-                for h in heads:
-                    rotate(j, (h,), upright, result)
-                    store(j, slice(h, h + 1), result)
+            together = len(ripe) == 2 and units[ripe[0]][0] == units[ripe[1]][0] and step < SLOTS - 1
+            if together:
+                j = units[ripe[0]][0]
+                rotate(j, (units[ripe[0]][1], units[ripe[1]][1]), upright, result_for(j), nc.gpsimd)
+                unstored.append((j, units[ripe[0]][1], 2))
             else:
-                rotate(j, heads, upright, result)
-            for grouped, first in fresh:
+                for n in ripe:
+                    j, h = units[n]
+                    rotate(j, (h,), upright, result_for(j), nc.vector if n == len(units) - 1 else nc.gpsimd)
+                    unstored.append((j, h, 1))
+            for grouped, first in turned_now:
                 quantise(grouped, first, 2)
-            if slot == 1:
+            if step == 1:
                 negate_first_half_of_sin(late)
-            if not last:
-                unstored.append((j, 2 * q))
             held = []
-            for block, first in unstored:
+            for block, first, count in unstored:
                 if done_tiles >= (block + 1) * BLOCK:
-                    store(block, slice(first, first + 2), result_of[block])
+                    store(block, slice(first, first + count), result_of[block])
                 else:
-                    held.append((block, first))
+                    held.append((block, first, count))
             unstored = held

@@ -44,6 +44,7 @@ def tile_gptossmlaattention_pb_kernel(tc, hidden_states, cos, sin, Wq_words, Wq_
     with ExitStack() as ctx:
         keep = ctx.enter_context(tc.tile_pool(name="keep", bufs=1))
         staging = ctx.enter_context(tc.tile_pool(name="staging", bufs=3))
+        sorting = ctx.enter_context(tc.tile_pool(name="sorting", bufs=2))
         channels = ctx.enter_context(tc.tile_pool(name="channels", bufs=4))
         scratch = ctx.enter_context(tc.tile_pool(name="scratch", bufs=3))
         results = ctx.enter_context(tc.tile_pool(name="results", bufs=3))
@@ -106,7 +107,16 @@ def tile_gptossmlaattention_pb_kernel(tc, hidden_states, cos, sin, Wq_words, Wq_
         for first in range(8, TILES, 2):
             load_x(slice(first, first + 2))
 
-        def turn(first, count):
+        def sort_words(first, count):
+            tidy = sorting.tile([P, count, HID // 2], F32, name="tidy")
+            for i in range(count):
+                nc.scalar.copy(
+                    out=tidy[:, i, :].rearrange("p (g u w) -> p g u w", g=PASSES, u=2),
+                    in_=x_sb[:, first + i, :].bitcast(F32).rearrange("p (g w u) -> p g u w", g=PASSES, u=2),
+                )
+            return tidy
+
+        def turn(first, count, tidy=None):
             grouped = staging.tile([P, PASSES, count * P * 4], BF16, align_bytes=64, name="grouped")
             grouped_words = grouped[:].bitcast(F32)
             for i in range(count):
@@ -115,12 +125,31 @@ def tile_gptossmlaattention_pb_kernel(tc, hidden_states, cos, sin, Wq_words, Wq_
                 for g in range(PASSES):
                     for u in range(2):
                         start = g * (K_PASS // 2) + u
-                        nc.tensor.transpose(flipped[:, 2 * g + u, :], x_words[:, start : (g + 1) * (K_PASS // 2) : 2], identity[:])
+                        if tidy is None:
+                            nc.tensor.transpose(flipped[:, 2 * g + u, :], x_words[:, start : (g + 1) * (K_PASS // 2) : 2], identity[:])
+                        else:
+                            nc.tensor.transpose(flipped[:, 2 * g + u, :], tidy[:, i, (2 * g + u) * P : (2 * g + u + 1) * P], identity[:])
                 nc.scalar.copy(
                     out=grouped_words[:, :, i * 2 * P : (i + 1) * 2 * P].rearrange("p g (r u) -> p g r u", u=2),
                     in_=flipped[:].rearrange("p (g u) r -> p g r u", u=2),
                 )
             return grouped
+
+        def turn_by_pass(t):
+            j, i = divmod(t, BLOCK)
+            columns = slice(i * P, (i + 1) * P)
+            x_words = x_sb[:, t, :].bitcast(F32)
+            grouped = staging.tile([P, PASSES, P * 4], BF16, align_bytes=64, name="grouped")
+            grouped_words = grouped[:].bitcast(F32)
+            for g in range(PASSES):
+                flipped = short.tile([P, 2, P], F32, name="brief")
+                for u in range(2):
+                    start = g * (K_PASS // 2) + u
+                    nc.tensor.transpose(flipped[:, u, :], x_words[:, start : (g + 1) * (K_PASS // 2) : 2], identity[:])
+                nc.scalar.copy(out=grouped_words[:, g, :].rearrange("p (r u) -> p r u", u=2), in_=flipped[:].rearrange("p u r -> p r u"))
+                nc.vector.quantize_mx(
+                    out=codes[j][:, g, columns].bitcast(FP8X4), scales=code_scales[j][:, g, columns], in_=grouped[:, g, :]
+                )
 
         def quantise(grouped, first, count):
             j, i = divmod(first, BLOCK)
@@ -190,6 +219,25 @@ def tile_gptossmlaattention_pb_kernel(tc, hidden_states, cos, sin, Wq_words, Wq_
                 op=ADD,
             )
 
+        def rotate_last(j, h, upright, result):
+            tiles = slice(j * BLOCK, (j + 1) * BLOCK)
+            products = scratch.tile([P, 2, 1, BLOCK, ROPE], F32, name="products")
+            nc.vector.tensor_tensor(
+                out=products[:, :, 0, :, :].rearrange("p r i d -> p r (i d)"),
+                in0=upright[h][:].rearrange("p i d -> p (i d)").unsqueeze(1).to_broadcast([P, 2, BLOCK * ROPE]),
+                in1=angles[:, :, tiles, :].rearrange("p r i d -> p r (i d)"),
+                op=MULT,
+            )
+            for first in range(0, BLOCK, 2):
+                rows = slice(first, first + 2)
+                nc.vector.tensor_tensor(
+                    out=result[:, h, rows, NOPE:HEAD].rearrange("p i (f d) -> p i f d", f=2),
+                    in0=products[:, 0, 0, rows, :].rearrange("p i (f d) -> p i f d", f=2),
+                    in1=products[:, 1, 0, rows, :].rearrange("p i (f d) -> p i f d", f=2)[:, :, ::-1, :],
+                    op=ADD,
+                )
+                nc.sync.dma_start(out=out_dram[:, h : h + 1, j * BLOCK + first : j * BLOCK + first + 2, :], in_=result[:, h : h + 1, rows, :])
+
         def negate_first_half_of_sin(tiles):
             nc.scalar.copy(out=angles[:, 1, tiles, 0:HALF], in_=sin_raw[:, tiles, HALF:ROPE])
             nc.scalar.mul(out=angles[:, 1, tiles, HALF:ROPE], in_=sin_raw[:, tiles, 0:HALF], mul=-1.0)
@@ -219,8 +267,9 @@ def tile_gptossmlaattention_pb_kernel(tc, hidden_states, cos, sin, Wq_words, Wq_
             else:
                 nc.gpsimd.tensor_tensor(out=place, in0=place, in1=bias_nope[:], op=ADD)
 
-        for t in range(BLOCK):
+        for t in range(BLOCK - 1):
             quantise(turn(t, 1), t, 1)
+        turn_by_pass(BLOCK - 1)
         spread = short.tile([P, HEADS, NOPE], F32, name="brief")
         nc.tensor.matmul(
             out=spread[:].rearrange("p h d -> p (h d)"),
@@ -265,6 +314,7 @@ def tile_gptossmlaattention_pb_kernel(tc, hidden_states, cos, sin, Wq_words, Wq_
             for h in range(HEADS):
                 units.append((j, h))
         by_channel = {}
+        tidy_of = {}
         unstored = []
         done_tiles = 0
         for step in range(SLOTS + 1):
@@ -284,13 +334,16 @@ def tile_gptossmlaattention_pb_kernel(tc, hidden_states, cos, sin, Wq_words, Wq_
             for t in flat:
                 if not on_vector(t):
                     copy_unrotated(t, unrotated[t])
+            for k in range(BLOCK, TILES // 2):
+                if turn_slot(k) == step + 1:
+                    tidy_of[k] = sort_words(2 * k, 2)
             upright = {}
             turned_now = []
             for n in ripe:
                 if n == 2 * step and step > 0:
                     for k in range(BLOCK // 2, TILES // 2):
                         if turn_slot(k) == step:
-                            turned_now.append((turn(2 * k, 2), 2 * k))
+                            turned_now.append((turn(2 * k, 2, tidy_of.get(k)), 2 * k))
                 upright[units[n][1]] = turn_back(by_channel[n])
             if step == 0:
                 turned_now.append((turn(BLOCK, 2), BLOCK))
@@ -305,8 +358,11 @@ def tile_gptossmlaattention_pb_kernel(tc, hidden_states, cos, sin, Wq_words, Wq_
             else:
                 for n in ripe:
                     j, h = units[n]
-                    rotate(j, (h,), upright, result_for(j), nc.vector if n == len(units) - 1 else nc.gpsimd)
-                    unstored.append((j, h, 1))
+                    if n == len(units) - 1:
+                        rotate_last(j, h, upright, result_for(j))
+                    else:
+                        rotate(j, (h,), upright, result_for(j), nc.gpsimd)
+                        unstored.append((j, h, 1))
             for grouped, first in turned_now:
                 quantise(grouped, first, 2)
             if step == 1:

@@ -253,19 +253,9 @@ def tile_gptossmlaattention_pb_kernel(tc, hidden_states, cos, sin, Wq_words, Wq_
                 result_of[j] = result
             return result_of[j]
 
-        def on_vector(t):
-            return t % BLOCK != 0
-
-        def copy_unrotated(t, bank):
-            place = result_for(t // BLOCK)[:, :, t % BLOCK, 0:NOPE]
-            nc.scalar.copy(out=place, in_=bank[:])
-
         def bias_unrotated(t, bank):
             place = result_for(t // BLOCK)[:, :, t % BLOCK, 0:NOPE]
-            if on_vector(t):
-                nc.vector.tensor_tensor(out=place, in0=bank[:], in1=bias_nope[:], op=ADD)
-            else:
-                nc.gpsimd.tensor_tensor(out=place, in0=place, in1=bias_nope[:], op=ADD)
+            nc.vector.tensor_tensor(out=place, in0=bank[:], in1=bias_nope[:], op=ADD)
 
         for t in range(BLOCK - 1):
             quantise(turn(t, 1), t, 1)
@@ -331,9 +321,6 @@ def tile_gptossmlaattention_pb_kernel(tc, hidden_states, cos, sin, Wq_words, Wq_
                 by_channel[n] = add_bias(units[n][1], banks[n])
             if step == 0:
                 negate_first_half_of_sin(early)
-            for t in flat:
-                if not on_vector(t):
-                    copy_unrotated(t, unrotated[t])
             for k in range(BLOCK, TILES // 2):
                 if turn_slot(k) == step + 1:
                     tidy_of[k] = sort_words(2 * k, 2)

@@ -26,10 +26,9 @@ COLS = HEADS * HEAD
 K_PASS = 4 * P
 PASSES = HID // K_PASS
 TILES = SEQ // P
-BLOCK = 4
-BLOCKS = TILES // BLOCK
-SLOTS_PER_BLOCK = HEADS // 2
-SLOTS = BLOCKS * SLOTS_PER_BLOCK
+BLOCK_TILES = (4, 4, 4, 4)
+UNIT = 512
+PIECES = UNIT // P
 
 FLOPS = 2 * SEQ * HID * COLS
 
@@ -40,6 +39,23 @@ def tile_gptossmlaattention_pb_kernel(tc, hidden_states, cos, sin, Wq_words, Wq_
     cos_dram = cos[0].rearrange("(p t) d -> p t d", t=TILES)
     sin_dram = sin[0].rearrange("(p t) d -> p t d", t=TILES)
     out_dram = out[0].rearrange("h (p t) d -> p h t d", t=TILES)
+
+    first_tile = []
+    block_of = []
+    for j, count in enumerate(BLOCK_TILES):
+        first_tile.append(len(block_of))
+        block_of.extend([j] * count)
+
+    units = []
+    for j, count in enumerate(BLOCK_TILES):
+        if count == 4:
+            for h in range(HEADS):
+                units.append((j, None, h, 1))
+        else:
+            for h in range(0, HEADS, PIECES):
+                for i in range(count):
+                    units.append((j, i, h, PIECES))
+    steps = len(units) // 2
 
     with ExitStack() as ctx:
         keep = ctx.enter_context(tc.tile_pool(name="keep", bufs=1))
@@ -54,7 +70,10 @@ def tile_gptossmlaattention_pb_kernel(tc, hidden_states, cos, sin, Wq_words, Wq_
         ctx.enter_context(tc.manual_schedule())
 
         x_sb = keep.tile([P, TILES, HID], BF16)
-        w_words = keep.tile([P, PASSES, 2 * COLS], U8, align_bytes=64)
+        w_words = []
+        for part in range(2):
+            part_words = keep.tile([P, PASSES, COLS], U8, align_bytes=64, name="w_words%d" % part)
+            w_words.append(part_words)
         w_scales = keep.tile([P, PASSES, COLS], U8, align_bytes=64)
         nope_words = keep.tile([P, PASSES, 2 * HEADS * NOPE], U8, align_bytes=64)
         nope_scales = keep.tile([P, PASSES, HEADS * NOPE], U8, align_bytes=64)
@@ -67,9 +86,10 @@ def tile_gptossmlaattention_pb_kernel(tc, hidden_states, cos, sin, Wq_words, Wq_
         identity = keep.tile([P, P], F32)
         codes = []
         code_scales = []
-        for j in range(BLOCKS):
-            block_codes = keep.tile([P, PASSES, BLOCK * P], U32, align_bytes=64, name="codes%d" % j)
-            block_scales = keep.tile([P, PASSES, BLOCK * P], U8, align_bytes=64, name="code_scales%d" % j)
+        for j, count in enumerate(BLOCK_TILES):
+            shape = [P, count, PASSES, P] if count == 2 else [P, PASSES, count, P]
+            block_codes = keep.tile(shape, U32, align_bytes=64, name="codes%d" % j)
+            block_scales = keep.tile(shape, U8, align_bytes=64, name="code_scales%d" % j)
             codes.append(block_codes)
             code_scales.append(block_scales)
 
@@ -85,89 +105,114 @@ def tile_gptossmlaattention_pb_kernel(tc, hidden_states, cos, sin, Wq_words, Wq_
             nc.sync.dma_start(out=angles[:, 0, tiles, :], in_=cos_dram[:, tiles, :])
             nc.sync.dma_start(out=sin_raw[:, tiles, :], in_=sin_dram[:, tiles, :])
 
-        early = slice(0, BLOCK)
-        late = slice(BLOCK, TILES)
-        for t in range(BLOCK):
+        early = slice(0, 4)
+        for t in range(4):
             load_x(slice(t, t + 1))
         nc.sync.dma_start(out=bias_row[0:1, :], in_=bq.unsqueeze(0))
-        for r in range(4):
-            nc.sync.dma_start(
-                out=w_scales[r:P:32].bitcast(I32),
-                in_=Wq_scales[:, r:16:4, :].rearrange("g q n -> q g n").bitcast(I32),
-            )
-        half_words = 2 * COLS // 8
-        w_sbuf = w_words[:].bitcast(I32)
-        w_dram = Wq_words.rearrange("g p n -> p g n").bitcast(I32)
-        nc.sync.dma_start(out=w_sbuf[:, :, 0:half_words], in_=w_dram[:, :, 0:half_words])
-        nc.sync.dma_start(out=w_sbuf[:, :, half_words:], in_=w_dram[:, :, half_words:])
+        def load_words(part):
+            columns = slice(part * (COLS // 2), (part + 1) * (COLS // 2))
+            for r in range(4):
+                nc.sync.dma_start(
+                    out=w_scales[r:P:32, :, columns].bitcast(I32),
+                    in_=Wq_scales[:, r:16:4, columns].rearrange("g q n -> q g n").bitcast(I32),
+                )
+            w_dram = Wq_words[:, :, part * COLS : (part + 1) * COLS]
+            nc.sync.dma_start(out=w_words[part][:].bitcast(I32), in_=w_dram.rearrange("g p n -> p g n").bitcast(I32))
+
+        load_words(0)
         load_angles(early)
-        load_x(slice(4, 6))
-        load_x(slice(6, 8))
-        load_angles(late)
-        for first in range(8, TILES, 2):
+        load_words(1)
+        for first in range(4, 8, 2):
+            load_x(slice(first, first + 2))
+        load_angles(slice(4, 8))
+        load_x(slice(8, 10))
+        load_x(slice(10, 12))
+        load_angles(slice(8, TILES))
+        for first in range(12, TILES, 2):
             load_x(slice(first, first + 2))
 
-        def sort_words(first, count):
-            tidy = sorting.tile([P, count, HID // 2], F32, name="tidy")
-            for i in range(count):
-                nc.scalar.copy(
-                    out=tidy[:, i, :].rearrange("p (g u w) -> p g u w", g=PASSES, u=2),
-                    in_=x_sb[:, first + i, :].bitcast(F32).rearrange("p (g w u) -> p g u w", g=PASSES, u=2),
-                )
-            return tidy
+        def words_of(t, g, u):
+            start = g * (K_PASS // 2) + u
+            return x_sb[:, t, :].bitcast(F32)[:, start : (g + 1) * (K_PASS // 2) : 2]
 
-        def turn(first, count, tidy=None):
-            grouped = staging.tile([P, PASSES, count * P * 4], BF16, align_bytes=64, name="grouped")
-            grouped_words = grouped[:].bitcast(F32)
-            for i in range(count):
-                x_words = x_sb[:, first + i, :].bitcast(F32)
-                flipped = short.tile([P, 2 * PASSES, P], F32, name="brief")
-                for g in range(PASSES):
-                    for u in range(2):
-                        start = g * (K_PASS // 2) + u
-                        if tidy is None:
-                            nc.tensor.transpose(flipped[:, 2 * g + u, :], x_words[:, start : (g + 1) * (K_PASS // 2) : 2], identity[:])
-                        else:
-                            nc.tensor.transpose(flipped[:, 2 * g + u, :], tidy[:, i, (2 * g + u) * P : (2 * g + u + 1) * P], identity[:])
-                nc.scalar.copy(
-                    out=grouped_words[:, :, i * 2 * P : (i + 1) * 2 * P].rearrange("p g (r u) -> p g r u", u=2),
-                    in_=flipped[:].rearrange("p (g u) r -> p g r u", u=2),
-                )
-            return grouped
+        def codes_of(j, i, g):
+            if BLOCK_TILES[j] == 2:
+                return codes[j][:, i, g, :].bitcast(FP8X4), code_scales[j][:, i, g, :]
+            return codes[j][:, g, i, :].bitcast(FP8X4), code_scales[j][:, g, i, :]
 
-        def turn_by_pass(t):
-            j, i = divmod(t, BLOCK)
-            columns = slice(i * P, (i + 1) * P)
-            x_words = x_sb[:, t, :].bitcast(F32)
+        def quantise_tile(j, i, grouped):
+            nc.vector.quantize_mx(
+                out=codes[j][:, i, :, :].rearrange("p g r -> p (g r)").bitcast(FP8X4),
+                scales=code_scales[j][:, i, :, :].rearrange("p g r -> p (g r)"),
+                in_=grouped,
+            )
+
+        def turn_first(t):
             grouped = staging.tile([P, PASSES, P * 4], BF16, align_bytes=64, name="grouped")
             grouped_words = grouped[:].bitcast(F32)
             for g in range(PASSES):
                 flipped = short.tile([P, 2, P], F32, name="brief")
                 for u in range(2):
-                    start = g * (K_PASS // 2) + u
-                    nc.tensor.transpose(flipped[:, u, :], x_words[:, start : (g + 1) * (K_PASS // 2) : 2], identity[:])
-                nc.scalar.copy(out=grouped_words[:, g, :].rearrange("p (r u) -> p r u", u=2), in_=flipped[:].rearrange("p u r -> p r u"))
-                nc.vector.quantize_mx(
-                    out=codes[j][:, g, columns].bitcast(FP8X4), scales=code_scales[j][:, g, columns], in_=grouped[:, g, :]
-                )
-
-        def quantise(grouped, first, count):
-            j, i = divmod(first, BLOCK)
-            columns = slice(i * P, (i + count) * P)
+                    nc.tensor.transpose(flipped[:, u, :], words_of(t, g, u), identity[:])
+                place = grouped_words[:, g, :].rearrange("p (r u) -> p r u", u=2)
+                if g == 0:
+                    nc.scalar.copy(out=place, in_=flipped[:].rearrange("p u r -> p r u"))
+                else:
+                    nc.vector.tensor_copy(out=place, in_=flipped[:].rearrange("p u r -> p r u"))
             for g in range(PASSES):
-                nc.vector.quantize_mx(
-                    out=codes[j][:, g, columns].bitcast(FP8X4), scales=code_scales[j][:, g, columns], in_=grouped[:, g, :]
-                )
+                words, scales = codes_of(0, t, g)
+                nc.vector.quantize_mx(out=words, scales=scales, in_=grouped[:, g, :])
+
+        def turn_tile(j, i):
+            grouped = staging.tile([P, PASSES * P * 4], BF16, align_bytes=64, name="grouped")
+            flipped = short.tile([P, PASSES, 2, P], F32, name="brief")
+            for g in range(PASSES):
+                for u in range(2):
+                    nc.tensor.transpose(flipped[:, g, u, :], words_of(first_tile[j] + i, g, u), identity[:])
+            nc.scalar.copy(
+                out=grouped[:].bitcast(F32).rearrange("p (g r u) -> p g r u", g=PASSES, u=2),
+                in_=flipped[:].rearrange("p g u r -> p g r u"),
+            )
+            return grouped
+
+        def turn_two(j, g, half, tidy, grouped):
+            flipped = short.tile([P, 2, 2, P], F32, name="brief")
+            for b in range(2):
+                for u in range(2):
+                    i = 2 * half + b
+                    source = words_of(first_tile[j] + i, g, u) if tidy is None else tidy[:, i, u, :]
+                    nc.tensor.transpose(flipped[:, b, u, :], source, identity[:])
+            nc.scalar.copy(
+                out=grouped[:, half, :].bitcast(F32).rearrange("p (b r u) -> p b r u", b=2, u=2),
+                in_=flipped[:].rearrange("p b u r -> p b r u"),
+            )
+
+        def sort_words(j, g):
+            count = BLOCK_TILES[j]
+            tiles = slice(first_tile[j], first_tile[j] + count)
+            tidy = sorting.tile([P, count, 2, P], F32, name="tidy")
+            nc.scalar.copy(
+                out=tidy[:],
+                in_=x_sb[:, tiles, g * K_PASS : (g + 1) * K_PASS].bitcast(F32).rearrange("p i (w u) -> p i u w", u=2),
+            )
+            return tidy
+
+        def quantise_pass(j, g, grouped):
+            nc.vector.quantize_mx(
+                out=codes[j][:, g, :, :].rearrange("p i r -> p (i r)").bitcast(FP8X4),
+                scales=code_scales[j][:, g, :, :].rearrange("p i r -> p (i r)"),
+                in_=grouped[:].rearrange("p h c -> p (h c)"),
+            )
 
         def multiply_unrotated(t):
-            j, i = divmod(t, BLOCK)
-            columns = slice(i * P, (i + 1) * P)
+            j = block_of[t]
             bank = short.tile([P, HEADS, NOPE], F32, name="brief")
             for g in range(PASSES):
+                words, scales = codes_of(j, t - first_tile[j], g)
                 nc.tensor.matmul_mx(
                     out=bank[:].rearrange("p h d -> p (h d)"),
-                    lhsT=codes[j][:, g, columns].bitcast(FP8X4),
-                    lhsT_scale=code_scales[j][:, g, columns],
+                    lhsT=words,
+                    lhsT_scale=scales,
                     rhs=nope_words[:, g, :].bitcast(FP4X4),
                     rhs_scale=nope_scales[:, g, :],
                     start=(g == 0),
@@ -175,91 +220,129 @@ def tile_gptossmlaattention_pb_kernel(tc, hidden_states, cos, sin, Wq_words, Wq_
                 )
             return bank
 
-        def multiply_rotated(j, h):
-            first = h * HEAD + NOPE
-            bank = sums.tile([P, BLOCK * P], F32, name="by_channel_sums")
-            for g in range(PASSES):
-                nc.tensor.matmul_mx(
-                    out=bank[:],
-                    lhsT=w_words[:, g, 2 * first : 2 * (first + ROPE)].bitcast(FP4X4),
-                    lhsT_scale=w_scales[:, g, first : first + ROPE],
-                    rhs=codes[j][:, g, :].bitcast(FP8X4),
-                    rhs_scale=code_scales[j][:, g, :],
-                    start=(g == 0),
-                    stop=(g == PASSES - 1),
-                )
+        def multiply_rotated(unit):
+            j, i, head, heads = unit
+            bank = sums.tile([P, heads, UNIT // heads], F32, name="by_channel_sums")
+            for n in range(heads):
+                first = (head + n) * HEAD + NOPE
+                part, inside = divmod(first, COLS // 2)
+                for g in range(PASSES):
+                    if i is None:
+                        words = codes[j][:, g, :, :].rearrange("p i r -> p (i r)").bitcast(FP8X4)
+                        scales = code_scales[j][:, g, :, :].rearrange("p i r -> p (i r)")
+                    else:
+                        words, scales = codes_of(j, i, g)
+                    nc.tensor.matmul_mx(
+                        out=bank[:, n, :],
+                        lhsT=w_words[part][:, g, 2 * inside : 2 * (inside + ROPE)].bitcast(FP4X4),
+                        lhsT_scale=w_scales[:, g, first : first + ROPE],
+                        rhs=words,
+                        rhs_scale=scales,
+                        start=(g == 0),
+                        stop=(g == PASSES - 1),
+                    )
             return bank
 
-        def add_bias(h, bank):
-            by_channel = channels.tile([P, BLOCK * P], F32, name="by_channel")
-            nc.scalar.activation(out=by_channel[:], in_=bank[:], func=IDENTITY, bias=bias_col[:, h : h + 1], scale=1.0)
+        def add_bias(unit, bank):
+            head, heads = unit[2], unit[3]
+            by_channel = channels.tile([P, heads, UNIT // heads], F32, name="by_channel")
+            for n in range(heads):
+                nc.scalar.activation(
+                    out=by_channel[:, n, :], in_=bank[:, n, :], func=IDENTITY, bias=bias_col[:, head + n : head + n + 1], scale=1.0
+                )
             return by_channel
 
         def turn_back(by_channel):
-            upright = back.tile([P, BLOCK, ROPE], F32, name="upright")
-            for i in range(BLOCK):
-                nc.tensor.transpose(upright[:, i, :], by_channel[:, i * P : (i + 1) * P], identity[:])
+            flat = by_channel[:].rearrange("p n x -> p (n x)")
+            upright = back.tile([P, PIECES, ROPE], F32, name="upright")
+            for i in range(PIECES):
+                nc.tensor.transpose(upright[:, i, :], flat[:, i * P : (i + 1) * P], identity[:])
             return upright
 
-        def rotate(j, heads, upright, result, adder):
-            tiles = slice(j * BLOCK, (j + 1) * BLOCK)
-            count = len(heads)
-            products = scratch.tile([P, 2, count, BLOCK, ROPE], F32, name="products")
-            for n in range(count):
+        def products_for(count):
+            products = scratch.tile([P, 2, count, UNIT], F32, name="products")
+            return products
+
+        def multiply_by_angles(unit, upright, products, m):
+            j, i, heads = unit[0], unit[1], unit[3]
+            if i is None:
                 nc.vector.tensor_tensor(
-                    out=products[:, :, n, :, :].rearrange("p r i d -> p r (i d)"),
-                    in0=upright[heads[n]][:].rearrange("p i d -> p (i d)").unsqueeze(1).to_broadcast([P, 2, BLOCK * ROPE]),
-                    in1=angles[:, :, tiles, :].rearrange("p r i d -> p r (i d)"),
+                    out=products[:, :, m, :],
+                    in0=upright[:].rearrange("p i d -> p (i d)").unsqueeze(1).to_broadcast([P, 2, UNIT]),
+                    in1=angles[:, :, first_tile[j] : first_tile[j] + BLOCK_TILES[j], :].rearrange("p r i d -> p r (i d)"),
                     op=MULT,
                 )
-            adder.tensor_tensor(
-                out=result[:, heads[0] : heads[0] + count, :, NOPE:HEAD].rearrange("p n i (f d) -> p (n i) f d", f=2),
-                in0=products[:, 0, :, :, :].rearrange("p n i (f d) -> p (n i) f d", f=2),
-                in1=products[:, 1, :, :, :].rearrange("p n i (f d) -> p (n i) f d", f=2)[:, :, ::-1, :],
+            else:
+                nc.vector.tensor_tensor(
+                    out=products[:].rearrange("p r m x -> p r (m x)").rearrange("p r (n i d) -> p r n i d", n=heads, d=ROPE)[:, :, :, i, :],
+                    in0=upright[:].unsqueeze(1).to_broadcast([P, 2, heads, ROPE]),
+                    in1=angles[:, :, first_tile[j] + i, :].unsqueeze(2).to_broadcast([P, 2, heads, ROPE]),
+                    op=MULT,
+                )
+
+        def add_products(group, products, result):
+            head = group[0][2]
+            heads = len(group) if group[0][1] is None else group[0][3]
+            nc.gpsimd.tensor_tensor(
+                out=result[:, head : head + heads, :, NOPE:HEAD].rearrange("p n i (f d) -> p (n i) f d", f=2),
+                in0=products[:, 0, :, :].rearrange("p m (a f d) -> p (m a) f d", f=2, d=HALF),
+                in1=products[:, 1, :, :].rearrange("p m (a f d) -> p (m a) f d", f=2, d=HALF)[:, :, ::-1, :],
                 op=ADD,
             )
 
-        def rotate_last(j, h, upright, result):
-            tiles = slice(j * BLOCK, (j + 1) * BLOCK)
-            products = scratch.tile([P, 2, 1, BLOCK, ROPE], F32, name="products")
-            nc.vector.tensor_tensor(
-                out=products[:, :, 0, :, :].rearrange("p r i d -> p r (i d)"),
-                in0=upright[h][:].rearrange("p i d -> p (i d)").unsqueeze(1).to_broadcast([P, 2, BLOCK * ROPE]),
-                in1=angles[:, :, tiles, :].rearrange("p r i d -> p r (i d)"),
-                op=MULT,
-            )
-            for first in range(0, BLOCK, 2):
+        def add_last(unit, products, result):
+            j, h = unit[0], unit[2]
+            split = products.rearrange("p r m (i f d) -> p (r m) i f d", f=2, d=HALF)
+            for first in range(0, BLOCK_TILES[j], 2):
                 rows = slice(first, first + 2)
                 nc.vector.tensor_tensor(
                     out=result[:, h, rows, NOPE:HEAD].rearrange("p i (f d) -> p i f d", f=2),
-                    in0=products[:, 0, 0, rows, :].rearrange("p i (f d) -> p i f d", f=2),
-                    in1=products[:, 1, 0, rows, :].rearrange("p i (f d) -> p i f d", f=2)[:, :, ::-1, :],
+                    in0=split[:, 0, rows, :, :],
+                    in1=split[:, 1, rows, ::-1, :],
                     op=ADD,
                 )
-                nc.sync.dma_start(out=out_dram[:, h : h + 1, j * BLOCK + first : j * BLOCK + first + 2, :], in_=result[:, h : h + 1, rows, :])
+                there = slice(first_tile[j] + first, first_tile[j] + first + 2)
+                nc.sync.dma_start(out=out_dram[:, h : h + 1, there, :], in_=result[:, h : h + 1, rows, :])
 
-        def negate_first_half_of_sin(tiles):
-            nc.scalar.copy(out=angles[:, 1, tiles, 0:HALF], in_=sin_raw[:, tiles, HALF:ROPE])
-            nc.scalar.mul(out=angles[:, 1, tiles, HALF:ROPE], in_=sin_raw[:, tiles, 0:HALF], mul=-1.0)
+        def negate_first_half_of_sin(tiles, engine):
+            if engine is nc.vector:
+                nc.vector.tensor_copy(out=angles[:, 1, tiles, 0:HALF], in_=sin_raw[:, tiles, HALF:ROPE])
+                nc.vector.tensor_scalar(out=angles[:, 1, tiles, HALF:ROPE], in0=sin_raw[:, tiles, 0:HALF], scalar1=-1.0, scalar2=None, op0=MULT)
+            else:
+                nc.scalar.copy(out=angles[:, 1, tiles, 0:HALF], in_=sin_raw[:, tiles, HALF:ROPE])
+                nc.scalar.mul(out=angles[:, 1, tiles, HALF:ROPE], in_=sin_raw[:, tiles, 0:HALF], mul=-1.0)
 
         def store(j, heads, result):
-            nc.sync.dma_start(out=out_dram[:, heads, j * BLOCK : (j + 1) * BLOCK, :], in_=result[:, heads, :, :])
+            there = slice(first_tile[j], first_tile[j] + BLOCK_TILES[j])
+            nc.sync.dma_start(out=out_dram[:, heads, there, :], in_=result[:, heads, :, :])
 
         result_of = {}
 
         def result_for(j):
             if j not in result_of:
-                result = results.tile([P, HEADS, BLOCK, HEAD], F32, name="result")
+                result = results.tile([P, HEADS, BLOCK_TILES[j], HEAD], F32, name="result")
                 result_of[j] = result
             return result_of[j]
 
-        def bias_unrotated(t, bank):
-            place = result_for(t // BLOCK)[:, :, t % BLOCK, 0:NOPE]
-            nc.vector.tensor_tensor(out=place, in0=bank[:], in1=bias_nope[:], op=ADD)
+        def copy_unrotated(t, bank):
+            j = block_of[t]
+            nc.scalar.copy(out=result_for(j)[:, :, t - first_tile[j], 0:NOPE], in_=bank[:])
 
-        for t in range(BLOCK - 1):
-            quantise(turn(t, 1), t, 1)
-        turn_by_pass(BLOCK - 1)
+        def bias_unrotated(t, bank, on_gpsimd):
+            j = block_of[t]
+            place = result_for(j)[:, :, t - first_tile[j], 0:NOPE]
+            if on_gpsimd:
+                nc.gpsimd.tensor_tensor(out=place, in0=place, in1=bias_nope[:], op=ADD)
+            else:
+                nc.vector.tensor_tensor(out=place, in0=bank[:], in1=bias_nope[:], op=ADD)
+
+        for t in range(BLOCK_TILES[0]):
+            turn_first(t)
+        stood = back.tile([P, HEADS], F32, name="upright")
+        for h in range(HEADS):
+            first = h * HEAD + NOPE
+            nc.tensor.matmul(out=stood[:, h : h + 1], lhsT=bias_row[:, first : first + ROPE], rhs=ones[:, 0:1], start=True, stop=True)
+        nc.scalar.copy(out=bias_col[:], in_=stood[:])
         spread = short.tile([P, HEADS, NOPE], F32, name="brief")
         nc.tensor.matmul(
             out=spread[:].rearrange("p h d -> p (h d)"),
@@ -268,95 +351,90 @@ def tile_gptossmlaattention_pb_kernel(tc, hidden_states, cos, sin, Wq_words, Wq_
             start=True,
             stop=True,
         )
-        nc.scalar.copy(out=bias_nope[:], in_=spread[:])
-        stood = back.tile([P, HEADS], F32, name="upright")
-        for h in range(HEADS):
-            first = h * HEAD + NOPE
-            nc.tensor.matmul(out=stood[:, h : h + 1], lhsT=bias_row[:, first : first + ROPE], rhs=ones[:, 0:1], start=True, stop=True)
-        nc.scalar.copy(out=bias_col[:], in_=stood[:])
-        nc.vector.tensor_copy(
-            out=nope_scales[:].bitcast(I32).rearrange("p g (h c) -> p g h c", h=HEADS),
-            in_=w_scales[:].bitcast(I32).rearrange("p g (h c) -> p g h c", h=HEADS)[:, :, :, 0 : NOPE // 4],
-        )
-        nc.vector.tensor_copy(
-            out=nope_words[:].bitcast(I32).rearrange("p g (h c) -> p g h c", h=HEADS),
-            in_=w_words[:].bitcast(I32).rearrange("p g (h c) -> p g h c", h=HEADS)[:, :, :, 0 : NOPE // 2],
-        )
+        nc.vector.tensor_copy(out=bias_nope[:], in_=spread[:])
 
-        def turn_slot(k):
-            return max(k - 2, 2 * k - 5)
+        def gather_unrotated_columns():
+            per_half = HEADS // 2
+            for part in range(2):
+                nc.gpsimd.tensor_copy(
+                    out=nope_words[:].bitcast(I32).rearrange("p g (h c) -> p g h c", h=HEADS)[:, :, part * per_half : (part + 1) * per_half, :],
+                    in_=w_words[part][:].bitcast(I32).rearrange("p g (h c) -> p g h c", h=per_half)[:, :, :, 0 : NOPE // 2],
+                )
+            nc.gpsimd.tensor_copy(
+                out=nope_scales[:].bitcast(I32).rearrange("p g (h c) -> p g h c", h=HEADS),
+                in_=w_scales[:].bitcast(I32).rearrange("p g (h c) -> p g h c", h=HEADS)[:, :, :, 0 : NOPE // 4],
+            )
 
-        turning_steps = []
-        for k in range(BLOCK // 2, TILES // 2):
-            turning_steps.append(turn_slot(k))
-        free_steps = []
-        for s in range(SLOTS):
-            if s not in turning_steps:
-                free_steps.append(s)
+        turned_in = {1: (1, 0), 2: (1, 1), 4: (2, 0), 5: (2, 1), 8: (3, 0), 9: (3, 1)}
+        FLAT_FROM = 1
+        FLAT = {s: (2 if s % 7 == 0 else 1) for s in range(1, 15)}
+        flat_in = {}
+        t = 0
+        for step in range(FLAT_FROM, steps):
+            count = min(FLAT.get(step, 0), TILES - t)
+            flat_in[step] = list(range(t, t + count))
+            t += count
+        negate_first_half_of_sin(early, nc.vector)
+        gather_unrotated_columns()
 
-        def unrotated_tiles(step):
-            if step in free_steps and 2 * free_steps.index(step) < TILES:
-                return [2 * free_steps.index(step), 2 * free_steps.index(step) + 1]
-            return []
-
-        units = []
-        for j in range(BLOCKS):
-            for h in range(HEADS):
-                units.append((j, h))
-        by_channel = {}
         tidy_of = {}
         unstored = []
         done_tiles = 0
-        for step in range(SLOTS + 1):
+        V_LAST = 2
+        LAG_FROM = 16
+        G_TILES = ()
+        by_channel = {}
+        for step in range(steps + 1):
             fresh = [n for n in (2 * step, 2 * step + 1) if n < len(units)]
-            ripe = [n for n in (2 * step - 1, 2 * step) if 0 <= n < len(units)]
-            flat = unrotated_tiles(step)
-            banks = {}
-            for n in fresh:
-                banks[n] = multiply_rotated(units[n][0], units[n][1])
-            unrotated = {}
-            for t in flat:
-                unrotated[t] = multiply_unrotated(t)
-            for n in fresh:
-                by_channel[n] = add_bias(units[n][1], banks[n])
-            if step == 0:
-                negate_first_half_of_sin(early)
-            for k in range(BLOCK, TILES // 2):
-                if turn_slot(k) == step + 1:
-                    tidy_of[k] = sort_words(2 * k, 2)
-            upright = {}
-            turned_now = []
-            for n in ripe:
-                if n == 2 * step and step > 0:
-                    for k in range(BLOCK // 2, TILES // 2):
-                        if turn_slot(k) == step:
-                            turned_now.append((turn(2 * k, 2, tidy_of.get(k)), 2 * k))
-                upright[units[n][1]] = turn_back(by_channel[n])
-            if step == 0:
-                turned_now.append((turn(BLOCK, 2), BLOCK))
-            for t in flat:
-                bias_unrotated(t, unrotated[t])
-                done_tiles = t + 1
-            together = len(ripe) == 2 and units[ripe[0]][0] == units[ripe[1]][0] and step < SLOTS - 1
-            if together:
-                j = units[ripe[0]][0]
-                rotate(j, (units[ripe[0]][1], units[ripe[1]][1]), upright, result_for(j), nc.gpsimd)
-                unstored.append((j, units[ripe[0]][1], 2))
-            else:
-                for n in ripe:
-                    j, h = units[n]
-                    if n == len(units) - 1:
-                        rotate_last(j, h, upright, result_for(j))
+            ripe = fresh
+            if step >= LAG_FROM:
+                ripe = [n for n in (2 * step - 1, 2 * step) if 2 * LAG_FROM <= n < len(units)]
+            chunk = turned_in.get(step, None)
+            flat = flat_in.get(step, [])
+            banks = [multiply_rotated(units[n]) for n in fresh]
+            unrotated = [multiply_unrotated(t) for t in flat]
+            for m in range(len(fresh)):
+                by_channel[fresh[m]] = add_bias(units[fresh[m]], banks[m])
+            for m in range(len(flat)):
+                if flat[m] in G_TILES:
+                    copy_unrotated(flat[m], unrotated[m])
+            soon = turned_in.get(step + 1, (0, None))
+            if soon[0] >= 2:
+                tidy_of[soon] = sort_words(soon[0], soon[1])
+            if chunk is not None:
+                both = staging.tile([P, 2, UNIT * 2], BF16, align_bytes=64, name="grouped")
+            uprights = []
+            for m in range(len(ripe)):
+                uprights.append(turn_back(by_channel[ripe[m]]))
+                if chunk is not None:
+                    turn_two(chunk[0], chunk[1], m, tidy_of.get(chunk, None), both)
+            for m in range(len(flat)):
+                bias_unrotated(flat[m], unrotated[m], flat[m] in G_TILES)
+                done_tiles = flat[m] + 1
+            if len(ripe) == 0:
+                continue
+            group = [units[n] for n in ripe]
+            j = group[0][0]
+            products = products_for(len(ripe))
+            for m in range(len(ripe)):
+                multiply_by_angles(group[m], uprights[m], products, m)
+            if step >= steps - 2:
+                for m in range(len(ripe)):
+                    if ripe[m] >= len(units) - V_LAST:
+                        add_last(group[m], products[:, :, m : m + 1, :], result_for(j))
                     else:
-                        rotate(j, (h,), upright, result_for(j), nc.gpsimd)
-                        unstored.append((j, h, 1))
-            for grouped, first in turned_now:
-                quantise(grouped, first, 2)
-            if step == 1:
-                negate_first_half_of_sin(late)
+                        add_products(group[m : m + 1], products[:, :, m : m + 1, :], result_for(j))
+                        unstored.append((j, group[m][2], 1))
+            else:
+                add_products(group, products, result_for(j))
+                unstored.append((j, group[0][2], len(group)))
+            if chunk is not None:
+                quantise_pass(chunk[0], chunk[1], both)
+            if step in (1, 3, 5):
+                negate_first_half_of_sin(slice(2 * step + 2, 2 * step + 6), nc.scalar)
             held = []
             for block, first, count in unstored:
-                if done_tiles >= (block + 1) * BLOCK:
+                if done_tiles >= first_tile[block] + BLOCK_TILES[block]:
                     store(block, slice(first, first + count), result_of[block])
                 else:
                     held.append((block, first, count))

from contextlib import ExitStack

import concourse.mybir as mybir
from concourse.masks import make_identity

F32 = mybir.dt.float32
BF16 = mybir.dt.bfloat16
I32 = mybir.dt.int32
U32 = mybir.dt.uint32
U8 = mybir.dt.uint8
FP8X4 = mybir.dt.float8_e4m3fn_x4
FP4X4 = mybir.dt.float4_e2m1fn_x4
ADD = mybir.AluOpType.add
MULT = mybir.AluOpType.mult
IDENTITY = mybir.ActivationFunctionType.Identity

P = 128
SEQ = 2048
HID = 1024
HEADS = 8
NOPE = 64
ROPE = 128
HALF = ROPE // 2
HEAD = NOPE + ROPE
COLS = HEADS * HEAD
K_PASS = 4 * P
PASSES = HID // K_PASS
TILES = SEQ // P
BLOCK_TILES = (4, 4, 4, 4)
UNIT = 512
PIECES = UNIT // P

FLOPS = 2 * SEQ * HID * COLS


def tile_gptossmlaattention_pb_kernel(tc, hidden_states, cos, sin, Wq_words, Wq_scales, bq, out):
    nc = tc.nc
    x_dram = hidden_states[0].rearrange("(p t) k -> p t k", t=TILES)
    cos_dram = cos[0].rearrange("(p t) d -> p t d", t=TILES)
    sin_dram = sin[0].rearrange("(p t) d -> p t d", t=TILES)
    out_dram = out[0].rearrange("h (p t) d -> p h t d", t=TILES)

    first_tile = []
    block_of = []
    for j, count in enumerate(BLOCK_TILES):
        first_tile.append(len(block_of))
        block_of.extend([j] * count)

    units = []
    for j, count in enumerate(BLOCK_TILES):
        if count == 4:
            for h in range(HEADS):
                units.append((j, None, h, 1))
        else:
            for h in range(0, HEADS, PIECES):
                for i in range(count):
                    units.append((j, i, h, PIECES))
    steps = len(units) // 2

    with ExitStack() as ctx:
        keep = ctx.enter_context(tc.tile_pool(name="keep", bufs=1))
        staging = ctx.enter_context(tc.tile_pool(name="staging", bufs=3))
        sorting = ctx.enter_context(tc.tile_pool(name="sorting", bufs=2))
        channels = ctx.enter_context(tc.tile_pool(name="channels", bufs=4))
        scratch = ctx.enter_context(tc.tile_pool(name="scratch", bufs=3))
        results = ctx.enter_context(tc.tile_pool(name="results", bufs=3))
        short = ctx.enter_context(tc.psum_pool(name="short", bufs=3))
        sums = ctx.enter_context(tc.psum_pool(name="sums", bufs=2))
        back = ctx.enter_context(tc.psum_pool(name="back", bufs=3))
        ctx.enter_context(tc.manual_schedule())

        x_sb = keep.tile([P, TILES, HID], BF16)
        w_words = []
        for part in range(2):
            part_words = keep.tile([P, PASSES, COLS], U8, align_bytes=64, name="w_words%d" % part)
            w_words.append(part_words)
        w_scales = keep.tile([P, PASSES, COLS], U8, align_bytes=64)
        nope_words = keep.tile([P, PASSES, 2 * HEADS * NOPE], U8, align_bytes=64)
        nope_scales = keep.tile([P, PASSES, HEADS * NOPE], U8, align_bytes=64)
        bias_row = keep.tile([P, COLS], BF16)
        ones = keep.tile([P, P], BF16)
        bias_nope = keep.tile([P, HEADS, NOPE], F32)
        bias_col = keep.tile([P, HEADS], F32)
        angles = keep.tile([P, 2, TILES, ROPE], BF16)
        sin_raw = keep.tile([P, TILES, ROPE], BF16)
        identity = keep.tile([P, P], F32)
        codes = []
        code_scales = []
        for j, count in enumerate(BLOCK_TILES):
            shape = [P, count, PASSES, P] if count == 2 else [P, PASSES, count, P]
            block_codes = keep.tile(shape, U32, align_bytes=64, name="codes%d" % j)
            block_scales = keep.tile(shape, U8, align_bytes=64, name="code_scales%d" % j)
            codes.append(block_codes)
            code_scales.append(block_scales)

        nc.vector.memset(bias_row[:].bitcast(I32), 0)
        nc.vector.memset(w_scales[:].bitcast(I32), 0)
        nc.vector.memset(ones[:], 1.0)
        make_identity(nc, identity[:])

        def load_x(tiles):
            nc.sync.dma_start(out=x_sb[:, tiles, :], in_=x_dram[:, tiles, :])

        def load_angles(tiles):
            nc.sync.dma_start(out=angles[:, 0, tiles, :], in_=cos_dram[:, tiles, :])
            nc.sync.dma_start(out=sin_raw[:, tiles, :], in_=sin_dram[:, tiles, :])

        early = slice(0, 4)
        for t in range(4):
            load_x(slice(t, t + 1))
        nc.sync.dma_start(out=bias_row[0:1, :], in_=bq.unsqueeze(0))
        def load_words(part):
            columns = slice(part * (COLS // 2), (part + 1) * (COLS // 2))
            for r in range(4):
                nc.sync.dma_start(
                    out=w_scales[r:P:32, :, columns].bitcast(I32),
                    in_=Wq_scales[:, r:16:4, columns].rearrange("g q n -> q g n").bitcast(I32),
                )
            w_dram = Wq_words[:, :, part * COLS : (part + 1) * COLS]
            nc.sync.dma_start(out=w_words[part][:].bitcast(I32), in_=w_dram.rearrange("g p n -> p g n").bitcast(I32))

        load_words(0)
        load_angles(early)
        load_words(1)
        for first in range(4, 8, 2):
            load_x(slice(first, first + 2))
        load_angles(slice(4, 8))
        load_x(slice(8, 10))
        load_x(slice(10, 12))
        load_angles(slice(8, TILES))
        for first in range(12, TILES, 2):
            load_x(slice(first, first + 2))

        def words_of(t, g, u):
            start = g * (K_PASS // 2) + u
            return x_sb[:, t, :].bitcast(F32)[:, start : (g + 1) * (K_PASS // 2) : 2]

        def codes_of(j, i, g):
            if BLOCK_TILES[j] == 2:
                return codes[j][:, i, g, :].bitcast(FP8X4), code_scales[j][:, i, g, :]
            return codes[j][:, g, i, :].bitcast(FP8X4), code_scales[j][:, g, i, :]

        def quantise_tile(j, i, grouped):
            nc.vector.quantize_mx(
                out=codes[j][:, i, :, :].rearrange("p g r -> p (g r)").bitcast(FP8X4),
                scales=code_scales[j][:, i, :, :].rearrange("p g r -> p (g r)"),
                in_=grouped,
            )

        def turn_first(t):
            grouped = staging.tile([P, PASSES, P * 4], BF16, align_bytes=64, name="grouped")
            grouped_words = grouped[:].bitcast(F32)
            for g in range(PASSES):
                flipped = short.tile([P, 2, P], F32, name="brief")
                for u in range(2):
                    nc.tensor.transpose(flipped[:, u, :], words_of(t, g, u), identity[:])
                place = grouped_words[:, g, :].rearrange("p (r u) -> p r u", u=2)
                if g == 0:
                    nc.scalar.copy(out=place, in_=flipped[:].rearrange("p u r -> p r u"))
                else:
                    nc.vector.tensor_copy(out=place, in_=flipped[:].rearrange("p u r -> p r u"))
            for g in range(PASSES):
                words, scales = codes_of(0, t, g)
                nc.vector.quantize_mx(out=words, scales=scales, in_=grouped[:, g, :])

        def turn_tile(j, i):
            grouped = staging.tile([P, PASSES * P * 4], BF16, align_bytes=64, name="grouped")
            flipped = short.tile([P, PASSES, 2, P], F32, name="brief")
            for g in range(PASSES):
                for u in range(2):
                    nc.tensor.transpose(flipped[:, g, u, :], words_of(first_tile[j] + i, g, u), identity[:])
            nc.scalar.copy(
                out=grouped[:].bitcast(F32).rearrange("p (g r u) -> p g r u", g=PASSES, u=2),
                in_=flipped[:].rearrange("p g u r -> p g r u"),
            )
            return grouped

        def turn_two(j, g, half, tidy, grouped):
            flipped = short.tile([P, 2, 2, P], F32, name="brief")
            for b in range(2):
                for u in range(2):
                    i = 2 * half + b
                    source = words_of(first_tile[j] + i, g, u) if tidy is None else tidy[:, i, u, :]
                    nc.tensor.transpose(flipped[:, b, u, :], source, identity[:])
            nc.scalar.copy(
                out=grouped[:, half, :].bitcast(F32).rearrange("p (b r u) -> p b r u", b=2, u=2),
                in_=flipped[:].rearrange("p b u r -> p b r u"),
            )

        def sort_words(j, g):
            count = BLOCK_TILES[j]
            tiles = slice(first_tile[j], first_tile[j] + count)
            tidy = sorting.tile([P, count, 2, P], F32, name="tidy")
            nc.scalar.copy(
                out=tidy[:],
                in_=x_sb[:, tiles, g * K_PASS : (g + 1) * K_PASS].bitcast(F32).rearrange("p i (w u) -> p i u w", u=2),
            )
            return tidy

        def quantise_pass(j, g, grouped):
            nc.vector.quantize_mx(
                out=codes[j][:, g, :, :].rearrange("p i r -> p (i r)").bitcast(FP8X4),
                scales=code_scales[j][:, g, :, :].rearrange("p i r -> p (i r)"),
                in_=grouped[:].rearrange("p h c -> p (h c)"),
            )

        def multiply_unrotated(t):
            j = block_of[t]
            bank = short.tile([P, HEADS, NOPE], F32, name="brief")
            for g in range(PASSES):
                words, scales = codes_of(j, t - first_tile[j], g)
                nc.tensor.matmul_mx(
                    out=bank[:].rearrange("p h d -> p (h d)"),
                    lhsT=words,
                    lhsT_scale=scales,
                    rhs=nope_words[:, g, :].bitcast(FP4X4),
                    rhs_scale=nope_scales[:, g, :],
                    start=(g == 0),
                    stop=(g == PASSES - 1),
                )
            return bank

        def multiply_rotated(unit):
            j, i, head, heads = unit
            bank = sums.tile([P, heads, UNIT // heads], F32, name="by_channel_sums")
            for n in range(heads):
                first = (head + n) * HEAD + NOPE
                part, inside = divmod(first, COLS // 2)
                for g in range(PASSES):
                    if i is None:
                        words = codes[j][:, g, :, :].rearrange("p i r -> p (i r)").bitcast(FP8X4)
                        scales = code_scales[j][:, g, :, :].rearrange("p i r -> p (i r)")
                    else:
                        words, scales = codes_of(j, i, g)
                    nc.tensor.matmul_mx(
                        out=bank[:, n, :],
                        lhsT=w_words[part][:, g, 2 * inside : 2 * (inside + ROPE)].bitcast(FP4X4),
                        lhsT_scale=w_scales[:, g, first : first + ROPE],
                        rhs=words,
                        rhs_scale=scales,
                        start=(g == 0),
                        stop=(g == PASSES - 1),
                    )
            return bank

        def add_bias(unit, bank):
            head, heads = unit[2], unit[3]
            by_channel = channels.tile([P, heads, UNIT // heads], F32, name="by_channel")
            for n in range(heads):
                nc.scalar.activation(
                    out=by_channel[:, n, :], in_=bank[:, n, :], func=IDENTITY, bias=bias_col[:, head + n : head + n + 1], scale=1.0
                )
            return by_channel

        def turn_back(by_channel):
            flat = by_channel[:].rearrange("p n x -> p (n x)")
            upright = back.tile([P, PIECES, ROPE], F32, name="upright")
            for i in range(PIECES):
                nc.tensor.transpose(upright[:, i, :], flat[:, i * P : (i + 1) * P], identity[:])
            return upright

        def products_for(count):
            products = scratch.tile([P, 2, count, UNIT], F32, name="products")
            return products

        def multiply_by_angles(unit, upright, products, m):
            j, i, heads = unit[0], unit[1], unit[3]
            if i is None:
                nc.vector.tensor_tensor(
                    out=products[:, :, m, :],
                    in0=upright[:].rearrange("p i d -> p (i d)").unsqueeze(1).to_broadcast([P, 2, UNIT]),
                    in1=angles[:, :, first_tile[j] : first_tile[j] + BLOCK_TILES[j], :].rearrange("p r i d -> p r (i d)"),
                    op=MULT,
                )
            else:
                nc.vector.tensor_tensor(
                    out=products[:].rearrange("p r m x -> p r (m x)").rearrange("p r (n i d) -> p r n i d", n=heads, d=ROPE)[:, :, :, i, :],
                    in0=upright[:].unsqueeze(1).to_broadcast([P, 2, heads, ROPE]),
                    in1=angles[:, :, first_tile[j] + i, :].unsqueeze(2).to_broadcast([P, 2, heads, ROPE]),
                    op=MULT,
                )

        def add_products(group, products, result):
            head = group[0][2]
            heads = len(group) if group[0][1] is None else group[0][3]
            nc.gpsimd.tensor_tensor(
                out=result[:, head : head + heads, :, NOPE:HEAD].rearrange("p n i (f d) -> p (n i) f d", f=2),
                in0=products[:, 0, :, :].rearrange("p m (a f d) -> p (m a) f d", f=2, d=HALF),
                in1=products[:, 1, :, :].rearrange("p m (a f d) -> p (m a) f d", f=2, d=HALF)[:, :, ::-1, :],
                op=ADD,
            )

        def add_last(unit, products, result):
            j, h = unit[0], unit[2]
            split = products.rearrange("p r m (i f d) -> p (r m) i f d", f=2, d=HALF)
            for first in range(0, BLOCK_TILES[j], 2):
                rows = slice(first, first + 2)
                nc.vector.tensor_tensor(
                    out=result[:, h, rows, NOPE:HEAD].rearrange("p i (f d) -> p i f d", f=2),
                    in0=split[:, 0, rows, :, :],
                    in1=split[:, 1, rows, ::-1, :],
                    op=ADD,
                )
                there = slice(first_tile[j] + first, first_tile[j] + first + 2)
                nc.sync.dma_start(out=out_dram[:, h : h + 1, there, :], in_=result[:, h : h + 1, rows, :])

        def negate_first_half_of_sin(tiles, engine):
            if engine is nc.vector:
                nc.vector.tensor_copy(out=angles[:, 1, tiles, 0:HALF], in_=sin_raw[:, tiles, HALF:ROPE])
                nc.vector.tensor_scalar(out=angles[:, 1, tiles, HALF:ROPE], in0=sin_raw[:, tiles, 0:HALF], scalar1=-1.0, scalar2=None, op0=MULT)
            else:
                nc.scalar.copy(out=angles[:, 1, tiles, 0:HALF], in_=sin_raw[:, tiles, HALF:ROPE])
                nc.scalar.mul(out=angles[:, 1, tiles, HALF:ROPE], in_=sin_raw[:, tiles, 0:HALF], mul=-1.0)

        def store(j, heads, result):
            there = slice(first_tile[j], first_tile[j] + BLOCK_TILES[j])
            nc.sync.dma_start(out=out_dram[:, heads, there, :], in_=result[:, heads, :, :])

        result_of = {}

        def result_for(j):
            if j not in result_of:
                result = results.tile([P, HEADS, BLOCK_TILES[j], HEAD], F32, name="result")
                result_of[j] = result
            return result_of[j]

        def copy_unrotated(t, bank):
            j = block_of[t]
            nc.scalar.copy(out=result_for(j)[:, :, t - first_tile[j], 0:NOPE], in_=bank[:])

        def bias_unrotated(t, bank, on_gpsimd):
            j = block_of[t]
            place = result_for(j)[:, :, t - first_tile[j], 0:NOPE]
            if on_gpsimd:
                nc.gpsimd.tensor_tensor(out=place, in0=place, in1=bias_nope[:], op=ADD)
            else:
                nc.vector.tensor_tensor(out=place, in0=bank[:], in1=bias_nope[:], op=ADD)

        for t in range(BLOCK_TILES[0]):
            turn_first(t)
        stood = back.tile([P, HEADS], F32, name="upright")
        for h in range(HEADS):
            first = h * HEAD + NOPE
            nc.tensor.matmul(out=stood[:, h : h + 1], lhsT=bias_row[:, first : first + ROPE], rhs=ones[:, 0:1], start=True, stop=True)
        nc.scalar.copy(out=bias_col[:], in_=stood[:])
        spread = short.tile([P, HEADS, NOPE], F32, name="brief")
        nc.tensor.matmul(
            out=spread[:].rearrange("p h d -> p (h d)"),
            lhsT=ones[:],
            rhs=bias_row[:].rearrange("p (h c) -> p h c", h=HEADS)[:, :, 0:NOPE],
            start=True,
            stop=True,
        )
        nc.vector.tensor_copy(out=bias_nope[:], in_=spread[:])

        def gather_unrotated_columns():
            per_half = HEADS // 2
            for part in range(2):
                nc.gpsimd.tensor_copy(
                    out=nope_words[:].bitcast(I32).rearrange("p g (h c) -> p g h c", h=HEADS)[:, :, part * per_half : (part + 1) * per_half, :],
                    in_=w_words[part][:].bitcast(I32).rearrange("p g (h c) -> p g h c", h=per_half)[:, :, :, 0 : NOPE // 2],
                )
            nc.gpsimd.tensor_copy(
                out=nope_scales[:].bitcast(I32).rearrange("p g (h c) -> p g h c", h=HEADS),
                in_=w_scales[:].bitcast(I32).rearrange("p g (h c) -> p g h c", h=HEADS)[:, :, :, 0 : NOPE // 4],
            )

        turned_in = {1: (1, 0), 2: (1, 1), 4: (2, 0), 5: (2, 1), 8: (3, 0), 9: (3, 1)}
        FLAT_FROM = 1
        FLAT = {s: (2 if s % 7 == 0 else 1) for s in range(1, 15)}
        flat_in = {}
        t = 0
        for step in range(FLAT_FROM, steps):
            count = min(FLAT.get(step, 0), TILES - t)
            flat_in[step] = list(range(t, t + count))
            t += count
        negate_first_half_of_sin(early, nc.vector)
        gather_unrotated_columns()

        tidy_of = {}
        unstored = []
        done_tiles = 0
        V_LAST = 2
        LAG_FROM = 16
        G_TILES = ()
        by_channel = {}
        for step in range(steps + 1):
            fresh = [n for n in (2 * step, 2 * step + 1) if n < len(units)]
            ripe = fresh
            if step >= LAG_FROM:
                ripe = [n for n in (2 * step - 1, 2 * step) if 2 * LAG_FROM <= n < len(units)]
            chunk = turned_in.get(step, None)
            flat = flat_in.get(step, [])
            banks = [multiply_rotated(units[n]) for n in fresh]
            unrotated = [multiply_unrotated(t) for t in flat]
            for m in range(len(fresh)):
                by_channel[fresh[m]] = add_bias(units[fresh[m]], banks[m])
            for m in range(len(flat)):
                if flat[m] in G_TILES:
                    copy_unrotated(flat[m], unrotated[m])
            soon = turned_in.get(step + 1, (0, None))
            if soon[0] >= 2:
                tidy_of[soon] = sort_words(soon[0], soon[1])
            if chunk is not None:
                both = staging.tile([P, 2, UNIT * 2], BF16, align_bytes=64, name="grouped")
            uprights = []
            for m in range(len(ripe)):
                uprights.append(turn_back(by_channel[ripe[m]]))
                if chunk is not None:
                    turn_two(chunk[0], chunk[1], m, tidy_of.get(chunk, None), both)
            for m in range(len(flat)):
                bias_unrotated(flat[m], unrotated[m], flat[m] in G_TILES)
                done_tiles = flat[m] + 1
            if len(ripe) == 0:
                continue
            group = [units[n] for n in ripe]
            j = group[0][0]
            products = products_for(len(ripe))
            for m in range(len(ripe)):
                multiply_by_angles(group[m], uprights[m], products, m)
            if step >= steps - 2:
                for m in range(len(ripe)):
                    if ripe[m] >= len(units) - V_LAST:
                        add_last(group[m], products[:, :, m : m + 1, :], result_for(j))
                    else:
                        add_products(group[m : m + 1], products[:, :, m : m + 1, :], result_for(j))
                        unstored.append((j, group[m][2], 1))
            else:
                add_products(group, products, result_for(j))
                unstored.append((j, group[0][2], len(group)))
            if chunk is not None:
                quantise_pass(chunk[0], chunk[1], both)
            if step in (1, 3, 5):
                negate_first_half_of_sin(slice(2 * step + 2, 2 * step + 6), nc.scalar)
            held = []
            for block, first, count in unstored:
                if done_tiles >= first_tile[block] + BLOCK_TILES[block]:
                    store(block, slice(first, first + count), result_of[block])
                else:
                    held.append((block, first, count))
            unstored = held
